import numpy as np
import ml_dtypes


def mxq(x, axis, fmt="e4m3"):
    dtype, down = {"e4m3": (ml_dtypes.float8_e4m3fn, 7), "e5m2": (ml_dtypes.float8_e5m2, 14)}[fmt]
    v = np.moveaxis(np.asarray(x, np.float32).astype(ml_dtypes.bfloat16).astype(np.float64), axis, -1)
    blocks = v.reshape(v.shape[:-1] + (-1, 32))
    amax = np.abs(blocks).max(-1, keepdims=True)
    byte = np.maximum(np.where(amax > 0, np.frexp(amax)[1] - 1 + 127, 0) - down, 1)
    scale = np.exp2(byte - 127.0)
    codes = (blocks / scale).astype(np.float32).astype(dtype).astype(np.float64)
    return np.moveaxis((codes * scale).reshape(v.shape), -1, axis)


WIDE = False


def mx_kscale(k):
    if not WIDE:
        return np.ones(k)
    levels = np.array([10, -10, 5, -5, 0])
    a = np.random.permutation(np.resize(levels, k // 512 * 4)).reshape(k // 512, 4)
    idx = np.arange(k)
    return np.exp2(a[idx // 512, idx % 128 // 32])


BF16 = ml_dtypes.bfloat16


def bf(x):
    return np.asarray(x, np.float32).astype(BF16)


def f64(x):
    return np.asarray(x).astype(np.float64)


B, C, E, H, HS, WS = 4, 512, 128, 4, 64, 64
N = HS * WS
CH = E // H
SCALE = (E / H) ** -0.5


def setup_inputs():
    s = mx_kscale(C)
    return {"xn": bf(np.random.standard_normal((B, C, HS, WS)) * s[None, :, None, None]),
            "Wqkv": bf(np.random.standard_normal((3 * E, C)) * 1.5 / np.sqrt(C) / s[None, :])}


def reference(xn, Wqkv):
    a = f64(xn).reshape(B, C, N)
    qkv = mxq(f64(Wqkv), 1, "e4m3") @ mxq(a, 1, "e4m3")
    q, k, v = [t.reshape(B, H, CH, N) for t in np.split(qkv, 3, axis=1)]
    eq = np.exp(q - q.max(axis=2, keepdims=True))
    q_soft = eq / eq.sum(axis=2, keepdims=True) * SCALE
    ek = np.exp(k - k.max(axis=3, keepdims=True))
    context = (mxq(ek, 3, "e4m3") @ mxq(v, 3, "e4m3").transpose(0, 1, 3, 2)) / ek.sum(axis=3, keepdims=True)
    return q_soft, context

@@ -1,0 +1,232 @@
+from contextlib import ExitStack
+
+import concourse.mybir as mybir
+from concourse.masks import make_identity
+
+BF16 = mybir.dt.bfloat16
+F32 = mybir.dt.float32
+U32 = mybir.dt.uint32
+U8 = mybir.dt.uint8
+FP8X4 = mybir.dt.float8_e4m3fn_x4
+ALU = mybir.AluOpType
+ACT = mybir.ActivationFunctionType
+AXIS_X = mybir.AxisListType.X
+
+P = 128
+PACK = 4
+BATCH = 4
+CHANNELS = 512
+POSITIONS = 4096
+EMBED = 128
+HEADS = 4
+HEAD_DIM = 32
+SCALE = HEAD_DIM**-0.5
+
+CHUNK = 512
+CHUNKS = POSITIONS // CHUNK
+SUBTILES = CHUNK // P
+GROUPS = SUBTILES * HEADS
+RUN = 4
+
+Q_ROWS, K_ROWS, V_ROWS = 0, 1, 2
+
+VECTOR_COLS = 160
+
+FLOPS = 2 * 3 * EMBED * CHANNELS * POSITIONS * BATCH + 2 * BATCH * HEADS * HEAD_DIM * HEAD_DIM * POSITIONS
+
+
+def tile_linearattention_pa_t_kernel(tc, xn, Wqkv, out_0, out_1):
+    nc = tc.nc
+    xn_view = xn.rearrange("b (t p) h w -> b p t (h w)", p=P)
+    q_soft_view = out_0.rearrange("b h c n -> b (h c) n")
+    context_view = out_1.rearrange("b h d f -> b (h d) f")
+
+    with ExitStack() as stack:
+        const = stack.enter_context(tc.tile_pool(name="const", bufs=1))
+        loads = stack.enter_context(tc.tile_pool(name="loads", bufs=6))
+        work = stack.enter_context(tc.tile_pool(name="work", bufs=3))
+        batch_pool = stack.enter_context(tc.tile_pool(name="batch", bufs=2))
+        psum = stack.enter_context(tc.psum_pool(name="psum", bufs=1))
+
+        ident_bf16 = const.tile([P, P], BF16)
+        make_identity(nc, ident_bf16[:])
+        ident_f32 = const.tile([P, P], F32)
+        make_identity(nc, ident_f32[:])
+
+        w_rows = const.tile([P, 3, CHANNELS], BF16)
+        nc.sync.dma_start(out=w_rows[:], in_=Wqkv.rearrange("(r p) c -> p r c", p=P))
+        w_grouped = const.tile([P, 3, EMBED, PACK], BF16, align_bytes=64)
+        w_codes = const.tile([P, 3, EMBED], U32, align_bytes=64)
+        w_scales = const.tile([P, 3, EMBED], U8, align_bytes=64)
+        for r in range(3):
+            w_t = psum.tile([P, PACK, P], BF16, tag="e_t")
+            for t in range(PACK):
+                nc.tensor.transpose(w_t[:, t, :], w_rows[:, r, t * P : (t + 1) * P], ident_bf16[:])
+            nc.vector.tensor_copy(out=w_grouped[:, r], in_=w_t[:].rearrange("p t m -> p m t"))
+            nc.vector.quantize_mx(
+                out=w_codes[:, r, :].bitcast(FP8X4),
+                scales=w_scales[:, r, :],
+                in_=w_grouped[:, r].rearrange("p m t -> p (m t)"),
+            )
+
+        state = {}
+
+        def channels_on_partitions(bank, rows, b, t):
+            cols = slice(t * CHUNK, (t + 1) * CHUNK)
+            nc.tensor.matmul_mx(
+                out=bank[:],
+                lhsT=w_codes[:, rows, :].bitcast(FP8X4),
+                lhsT_scale=w_scales[:, rows, :],
+                rhs=state["x_codes", b][:, cols].bitcast(FP8X4),
+                rhs_scale=state["x_scales", b][:, cols],
+                start=True,
+                stop=True,
+            )
+
+        def positions_on_partitions(bank, rows, b, t):
+            for j in range(SUBTILES):
+                tile_cols = slice(t * CHUNK + j * P, t * CHUNK + (j + 1) * P)
+                nc.tensor.matmul_mx(
+                    out=bank[:, j, :],
+                    lhsT=state["x_codes", b][:, tile_cols].bitcast(FP8X4),
+                    lhsT_scale=state["x_scales", b][:, tile_cols],
+                    rhs=w_codes[:, rows, :].bitcast(FP8X4),
+                    rhs_scale=w_scales[:, rows, :],
+                    start=True,
+                    stop=True,
+                )
+
+        def first_pass(b, t):
+            if t == 0:
+                state["x_codes", b] = batch_pool.tile([P, POSITIONS], U32, align_bytes=64, name="x_codes")
+                state["x_scales", b] = batch_pool.tile([P, POSITIONS], U8, align_bytes=64, name="x_scales")
+                state["v_codes", b] = batch_pool.tile([P, CHUNKS, EMBED], U32, align_bytes=64, name="v_codes")
+                state["v_scales", b] = batch_pool.tile([P, CHUNKS, EMBED], U8, align_bytes=64, name="v_scales")
+                state["k_max", b] = batch_pool.tile([P, CHUNKS], F32, name="k_max")
+            x_codes, x_scales = state["x_codes", b], state["x_scales", b]
+            cols = slice(t * CHUNK, (t + 1) * CHUNK)
+            x_raw = loads.tile([P, PACK, CHUNK], BF16)
+            nc.sync.dma_start(out=x_raw[:], in_=xn_view[b, :, :, cols])
+
+            x_grouped = work.tile([P, CHUNK, PACK], BF16, align_bytes=64)
+            nc.vector.tensor_copy(
+                out=x_grouped[:, :VECTOR_COLS, :].rearrange("p (n i) t -> p n t i", i=RUN),
+                in_=x_raw[:, :, :VECTOR_COLS].rearrange("p t (n i) -> p n t i", i=RUN),
+            )
+            nc.scalar.copy(
+                out=x_grouped[:, VECTOR_COLS:, :].rearrange("p (n i) t -> p n t i", i=RUN),
+                in_=x_raw[:, :, VECTOR_COLS:].rearrange("p t (n i) -> p n t i", i=RUN),
+            )
+            nc.vector.quantize_mx(
+                out=x_codes[:, cols].bitcast(FP8X4),
+                scales=x_scales[:, cols],
+                in_=x_grouped[:].rearrange("p n t -> p (n t)"),
+            )
+
+            k_first = psum.tile([P, CHUNK], F32, tag="k_first")
+            channels_on_partitions(k_first, K_ROWS, b, t)
+            nc.vector.tensor_reduce(out=state["k_max", b][:, t : t + 1], in_=k_first[:], axis=AXIS_X, op=ALU.max)
+
+            v_t = psum.tile([P, SUBTILES, EMBED], F32, tag="v_t")
+            positions_on_partitions(v_t, V_ROWS, b, t)
+            v_grouped = work.tile([P, EMBED, PACK], BF16, align_bytes=64)
+            nc.scalar.copy(out=v_grouped[:], in_=v_t[:].rearrange("p j m -> p m j"))
+            nc.vector.quantize_mx(
+                out=state["v_codes", b][:, t, :].bitcast(FP8X4),
+                scales=state["v_scales", b][:, t, :],
+                in_=v_grouped[:].rearrange("p m j -> p (m j)"),
+            )
+
+        def second_pass(b, t):
+            if t == 0:
+                k_top = batch_pool.tile([P, 1], F32, name="k_top")
+                nc.vector.tensor_reduce(out=k_top[:], in_=state["k_max", b][:], axis=AXIS_X, op=ALU.max)
+                minus_k_top = batch_pool.tile([P, 1], F32, name="minus_k_top")
+                nc.vector.tensor_scalar_mul(out=minus_k_top[:], in0=k_top[:], scalar1=-1.0)
+                state["minus_k_top"] = minus_k_top
+                state["e_sums"] = batch_pool.tile([P, CHUNKS], F32, name="e_sums")
+                state["context"] = psum.tile([P, EMBED], F32, tag="context", name="context")
+            cols = slice(t * CHUNK, (t + 1) * CHUNK)
+
+            q_t = psum.tile([P, SUBTILES, EMBED], F32, tag="q_t", bufs=2)
+            positions_on_partitions(q_t, Q_ROWS, b, t)
+            q_groups = q_t[:].rearrange("p j (h c) -> p (j h) c", c=HEAD_DIM)
+            q_max = work.tile([P, GROUPS], F32)
+            nc.vector.tensor_reduce(out=q_max[:], in_=q_groups, axis=AXIS_X, op=ALU.max)
+            q_exp = work.tile([P, GROUPS, HEAD_DIM], F32)
+            nc.vector.tensor_tensor(
+                out=q_exp[:],
+                in0=q_groups,
+                in1=q_max[:].unsqueeze(2).to_broadcast([P, GROUPS, HEAD_DIM]),
+                op=ALU.subtract,
+            )
+            nc.scalar.activation(out=q_exp[:], in_=q_exp[:], func=ACT.Exp)
+            q_sum = work.tile([P, GROUPS], F32)
+            nc.vector.tensor_reduce(out=q_sum[:], in_=q_exp[:], axis=AXIS_X, op=ALU.add)
+            q_inv = work.tile([P, GROUPS], F32)
+            nc.vector.reciprocal(out=q_inv[:], in_=q_sum[:])
+            q_norm = work.tile([P, GROUPS, HEAD_DIM], F32)
+            nc.vector.tensor_tensor(
+                out=q_norm[:],
+                in0=q_exp[:],
+                in1=q_inv[:].unsqueeze(2).to_broadcast([P, GROUPS, HEAD_DIM]),
+                op=ALU.mult,
+            )
+            q_back = psum.tile([P, SUBTILES, P], F32, tag="q_back")
+            q_tiles = q_norm[:].rearrange("p (j h) c -> p j (h c)", h=HEADS)
+            for j in range(SUBTILES):
+                nc.tensor.transpose(q_back[:, j, :], q_tiles[:, j, :], ident_f32[:])
+            q_out = loads.tile([P, CHUNK], F32)
+            nc.scalar.mul(out=q_out[:], in_=q_back[:].rearrange("p j n -> p (j n)"), mul=SCALE)
+            nc.sync.dma_start(out=q_soft_view[b, :, cols], in_=q_out[:])
+
+            k_again = psum.tile([P, CHUNK], F32, tag="k_again")
+            channels_on_partitions(k_again, K_ROWS, b, t)
+            e_rows = work.tile([P, CHUNK], BF16)
+            nc.scalar.activation(
+                out=e_rows[:],
+                in_=k_again[:],
+                func=ACT.Exp,
+                bias=state["minus_k_top"][:],
+                scale=1.0,
+                accum_out=state["e_sums"][:, t : t + 1],
+            )
+            e_t = psum.tile([P, SUBTILES, EMBED], BF16, tag="e_t")
+            for j in range(SUBTILES):
+                nc.tensor.transpose(e_t[:, j, :], e_rows[:, j * P : (j + 1) * P], ident_bf16[:])
+            e_grouped = work.tile([P, EMBED, PACK], BF16, align_bytes=64)
+            nc.scalar.copy(out=e_grouped[:], in_=e_t[:].rearrange("p j m -> p m j"))
+            e_codes = work.tile([P, EMBED], U32, align_bytes=64)
+            e_scales = work.tile([P, EMBED], U8, align_bytes=64)
+            nc.vector.quantize_mx(
+                out=e_codes[:].bitcast(FP8X4), scales=e_scales[:], in_=e_grouped[:].rearrange("p m j -> p (m j)")
+            )
+            context = state["context"]
+            nc.tensor.matmul_mx(
+                out=context[:],
+                lhsT=e_codes[:].bitcast(FP8X4),
+                lhsT_scale=e_scales[:],
+                rhs=state["v_codes", b][:, t, :].bitcast(FP8X4),
+                rhs_scale=state["v_scales", b][:, t, :],
+                start=(t == 0),
+                stop=(t == CHUNKS - 1),
+            )
+            if t == CHUNKS - 1:
+                e_total = batch_pool.tile([P, 1], F32, name="e_total")
+                nc.vector.tensor_reduce(out=e_total[:], in_=state["e_sums"][:], axis=AXIS_X, op=ALU.add)
+                e_inv = batch_pool.tile([P, 1], F32, name="e_inv")
+                nc.vector.reciprocal(out=e_inv[:], in_=e_total[:])
+                context_out = batch_pool.tile([P, HEAD_DIM], F32, name="context_out")
+                for h in range(HEADS):
+                    rows = slice(h * HEAD_DIM, (h + 1) * HEAD_DIM)
+                    nc.vector.tensor_scalar_mul(
+                        out=context_out[rows, :], in0=context[rows, rows], scalar1=e_inv[rows, :]
+                    )
+                nc.sync.dma_start(out=context_view[b], in_=context_out[:])
+
+        steps = BATCH * CHUNKS
+        for step in range(steps + CHUNKS):
+            if step < steps:
+                first_pass(step // CHUNKS, step % CHUNKS)
+            if step >= CHUNKS:
+                second_pass((step - CHUNKS) // CHUNKS, (step - CHUNKS) % CHUNKS)

@@ -30,6 +30,9 @@ RUN = 4
 
 Q_ROWS, K_ROWS, V_ROWS = 0, 1, 2
 
+SECOND_PASS_LAG = CHUNKS + 2
+PREFETCH = 4
+
 VECTOR_COLS = 160
 
 FLOPS = 2 * 3 * EMBED * CHANNELS * POSITIONS * BATCH + 2 * BATCH * HEADS * HEAD_DIM * HEAD_DIM * POSITIONS
@@ -44,9 +47,10 @@ def tile_linearattention_pa_t_kernel(tc, xn, Wqkv, out_0, out_1):
     with ExitStack() as stack:
         const = stack.enter_context(tc.tile_pool(name="const", bufs=1))
         loads = stack.enter_context(tc.tile_pool(name="loads", bufs=6))
-        work = stack.enter_context(tc.tile_pool(name="work", bufs=3))
+        work = stack.enter_context(tc.tile_pool(name="work", bufs=4))
         batch_pool = stack.enter_context(tc.tile_pool(name="batch", bufs=2))
         psum = stack.enter_context(tc.psum_pool(name="psum", bufs=1))
+        stack.enter_context(tc.manual_schedule())
 
         ident_bf16 = const.tile([P, P], BF16)
         make_identity(nc, ident_bf16[:])
@@ -69,164 +73,251 @@ def tile_linearattention_pa_t_kernel(tc, xn, Wqkv, out_0, out_1):
                 in_=w_grouped[:, r].rearrange("p m t -> p (m t)"),
             )
 
-        state = {}
+        TOTAL = BATCH * CHUNKS
+        tiles = {}
 
-        def channels_on_partitions(bank, rows, b, t):
-            cols = slice(t * CHUNK, (t + 1) * CHUNK)
+        def columns(i):
+            return slice((i % CHUNKS) * CHUNK, (i % CHUNKS + 1) * CHUNK)
+
+        def channels_on_partitions(bank, rows, i):
             nc.tensor.matmul_mx(
                 out=bank[:],
                 lhsT=w_codes[:, rows, :].bitcast(FP8X4),
                 lhsT_scale=w_scales[:, rows, :],
-                rhs=state["x_codes", b][:, cols].bitcast(FP8X4),
-                rhs_scale=state["x_scales", b][:, cols],
+                rhs=tiles["x_codes", i // CHUNKS][:, columns(i)].bitcast(FP8X4),
+                rhs_scale=tiles["x_scales", i // CHUNKS][:, columns(i)],
                 start=True,
                 stop=True,
             )
 
-        def positions_on_partitions(bank, rows, b, t):
+        def positions_on_partitions(bank, rows, i):
             for j in range(SUBTILES):
-                tile_cols = slice(t * CHUNK + j * P, t * CHUNK + (j + 1) * P)
+                first = (i % CHUNKS) * CHUNK + j * P
                 nc.tensor.matmul_mx(
                     out=bank[:, j, :],
-                    lhsT=state["x_codes", b][:, tile_cols].bitcast(FP8X4),
-                    lhsT_scale=state["x_scales", b][:, tile_cols],
+                    lhsT=tiles["x_codes", i // CHUNKS][:, first : first + P].bitcast(FP8X4),
+                    lhsT_scale=tiles["x_scales", i // CHUNKS][:, first : first + P],
                     rhs=w_codes[:, rows, :].bitcast(FP8X4),
                     rhs_scale=w_scales[:, rows, :],
                     start=True,
                     stop=True,
                 )
 
-        def first_pass(b, t):
-            if t == 0:
-                state["x_codes", b] = batch_pool.tile([P, POSITIONS], U32, align_bytes=64, name="x_codes")
-                state["x_scales", b] = batch_pool.tile([P, POSITIONS], U8, align_bytes=64, name="x_scales")
-                state["v_codes", b] = batch_pool.tile([P, CHUNKS, EMBED], U32, align_bytes=64, name="v_codes")
-                state["v_scales", b] = batch_pool.tile([P, CHUNKS, EMBED], U8, align_bytes=64, name="v_scales")
-                state["k_max", b] = batch_pool.tile([P, CHUNKS], F32, name="k_max")
-            x_codes, x_scales = state["x_codes", b], state["x_scales", b]
-            cols = slice(t * CHUNK, (t + 1) * CHUNK)
-            x_raw = loads.tile([P, PACK, CHUNK], BF16)
-            nc.sync.dma_start(out=x_raw[:], in_=xn_view[b, :, :, cols])
+        def load_x(i):
+            x_raw = loads.tile([P, PACK, CHUNK], BF16, name="x_raw")
+            nc.sync.dma_start(out=x_raw[:], in_=xn_view[i // CHUNKS, :, :, columns(i)])
+            tiles["x_raw", i] = x_raw
 
-            x_grouped = work.tile([P, CHUNK, PACK], BF16, align_bytes=64)
+        def regroup_x_vector(i):
+            x_grouped = work.tile([P, CHUNK, PACK], BF16, align_bytes=64, name="x_grouped")
+            tiles["x_grouped", i] = x_grouped
             nc.vector.tensor_copy(
                 out=x_grouped[:, :VECTOR_COLS, :].rearrange("p (n i) t -> p n t i", i=RUN),
-                in_=x_raw[:, :, :VECTOR_COLS].rearrange("p t (n i) -> p n t i", i=RUN),
+                in_=tiles["x_raw", i][:, :, :VECTOR_COLS].rearrange("p t (n i) -> p n t i", i=RUN),
             )
+
+        def regroup_x_scalar(i):
             nc.scalar.copy(
-                out=x_grouped[:, VECTOR_COLS:, :].rearrange("p (n i) t -> p n t i", i=RUN),
-                in_=x_raw[:, :, VECTOR_COLS:].rearrange("p t (n i) -> p n t i", i=RUN),
+                out=tiles["x_grouped", i][:, VECTOR_COLS:, :].rearrange("p (n i) t -> p n t i", i=RUN),
+                in_=tiles["x_raw", i][:, :, VECTOR_COLS:].rearrange("p t (n i) -> p n t i", i=RUN),
             )
+
+        def quantise_x(i):
+            b = i // CHUNKS
+            if i % CHUNKS == 0:
+                tiles["x_codes", b] = batch_pool.tile([P, POSITIONS], U32, align_bytes=64, name="x_codes")
+                tiles["x_scales", b] = batch_pool.tile([P, POSITIONS], U8, align_bytes=64, name="x_scales")
+                tiles["v_codes", b] = batch_pool.tile([P, CHUNKS, EMBED], U32, align_bytes=64, name="v_codes", bufs=3)
+                tiles["v_scales", b] = batch_pool.tile([P, CHUNKS, EMBED], U8, align_bytes=64, name="v_scales", bufs=3)
+                tiles["k_max", b] = batch_pool.tile([P, CHUNKS], F32, name="k_max")
             nc.vector.quantize_mx(
-                out=x_codes[:, cols].bitcast(FP8X4),
-                scales=x_scales[:, cols],
-                in_=x_grouped[:].rearrange("p n t -> p (n t)"),
+                out=tiles["x_codes", b][:, columns(i)].bitcast(FP8X4),
+                scales=tiles["x_scales", b][:, columns(i)],
+                in_=tiles["x_grouped", i][:].rearrange("p n t -> p (n t)"),
             )
 
-            k_first = psum.tile([P, CHUNK], F32, tag="k_first")
-            channels_on_partitions(k_first, K_ROWS, b, t)
-            nc.vector.tensor_reduce(out=state["k_max", b][:, t : t + 1], in_=k_first[:], axis=AXIS_X, op=ALU.max)
+        def matmul_k_first_and_v(i):
+            k_first = psum.tile([P, CHUNK], F32, tag="k_first", name="k_first")
+            channels_on_partitions(k_first, K_ROWS, i)
+            tiles["k_first", i] = k_first
+            v_t = psum.tile([P, SUBTILES, EMBED], F32, tag="v_t", name="v_t")
+            positions_on_partitions(v_t, V_ROWS, i)
+            tiles["v_t", i] = v_t
 
-            v_t = psum.tile([P, SUBTILES, EMBED], F32, tag="v_t")
-            positions_on_partitions(v_t, V_ROWS, b, t)
-            v_grouped = work.tile([P, EMBED, PACK], BF16, align_bytes=64)
-            nc.scalar.copy(out=v_grouped[:], in_=v_t[:].rearrange("p j m -> p m j"))
-            nc.vector.quantize_mx(
-                out=state["v_codes", b][:, t, :].bitcast(FP8X4),
-                scales=state["v_scales", b][:, t, :],
-                in_=v_grouped[:].rearrange("p m j -> p (m j)"),
+        def maximum_of_k(i):
+            b, t = i // CHUNKS, i % CHUNKS
+            nc.vector.tensor_reduce(
+                out=tiles["k_max", b][:, t : t + 1], in_=tiles["k_first", i][:], axis=AXIS_X, op=ALU.max
             )
-
-        def second_pass(b, t):
-            if t == 0:
+            if t == CHUNKS - 1:
                 k_top = batch_pool.tile([P, 1], F32, name="k_top")
-                nc.vector.tensor_reduce(out=k_top[:], in_=state["k_max", b][:], axis=AXIS_X, op=ALU.max)
+                nc.vector.tensor_reduce(out=k_top[:], in_=tiles["k_max", b][:], axis=AXIS_X, op=ALU.max)
                 minus_k_top = batch_pool.tile([P, 1], F32, name="minus_k_top")
                 nc.vector.tensor_scalar_mul(out=minus_k_top[:], in0=k_top[:], scalar1=-1.0)
-                state["minus_k_top"] = minus_k_top
-                state["e_sums"] = batch_pool.tile([P, CHUNKS], F32, name="e_sums")
-                state["context"] = psum.tile([P, EMBED], F32, tag="context", name="context")
-            cols = slice(t * CHUNK, (t + 1) * CHUNK)
+                tiles["minus_k_top", b] = minus_k_top
 
-            q_t = psum.tile([P, SUBTILES, EMBED], F32, tag="q_t", bufs=2)
-            positions_on_partitions(q_t, Q_ROWS, b, t)
-            q_groups = q_t[:].rearrange("p j (h c) -> p (j h) c", c=HEAD_DIM)
-            q_max = work.tile([P, GROUPS], F32)
-            nc.vector.tensor_reduce(out=q_max[:], in_=q_groups, axis=AXIS_X, op=ALU.max)
-            q_exp = work.tile([P, GROUPS, HEAD_DIM], F32)
-            nc.vector.tensor_tensor(
-                out=q_exp[:],
-                in0=q_groups,
-                in1=q_max[:].unsqueeze(2).to_broadcast([P, GROUPS, HEAD_DIM]),
-                op=ALU.subtract,
+        def copy_out_v(i):
+            v_grouped = work.tile([P, EMBED, PACK], BF16, align_bytes=64, name="v_grouped")
+            nc.scalar.copy(out=v_grouped[:], in_=tiles["v_t", i][:].rearrange("p j m -> p m j"))
+            tiles["v_grouped", i] = v_grouped
+
+        def quantise_v(i):
+            b, t = i // CHUNKS, i % CHUNKS
+            nc.vector.quantize_mx(
+                out=tiles["v_codes", b][:, t, :].bitcast(FP8X4),
+                scales=tiles["v_scales", b][:, t, :],
+                in_=tiles["v_grouped", i][:].rearrange("p m j -> p (m j)"),
             )
-            nc.scalar.activation(out=q_exp[:], in_=q_exp[:], func=ACT.Exp)
-            q_sum = work.tile([P, GROUPS], F32)
-            nc.vector.tensor_reduce(out=q_sum[:], in_=q_exp[:], axis=AXIS_X, op=ALU.add)
-            q_inv = work.tile([P, GROUPS], F32)
-            nc.vector.reciprocal(out=q_inv[:], in_=q_sum[:])
-            q_norm = work.tile([P, GROUPS, HEAD_DIM], F32)
-            nc.vector.tensor_tensor(
-                out=q_norm[:],
-                in0=q_exp[:],
-                in1=q_inv[:].unsqueeze(2).to_broadcast([P, GROUPS, HEAD_DIM]),
-                op=ALU.mult,
-            )
-            q_back = psum.tile([P, SUBTILES, P], F32, tag="q_back")
-            q_tiles = q_norm[:].rearrange("p (j h) c -> p j (h c)", h=HEADS)
+
+        def spread(per_group):
+            return per_group[:].unsqueeze(2).to_broadcast([P, GROUPS, HEAD_DIM])
+
+        def matmul_q(i):
+            q_t = psum.tile([P, SUBTILES, EMBED], F32, tag="q_t", bufs=2, name="q_t")
+            positions_on_partitions(q_t, Q_ROWS, i)
+            tiles["q_t", i] = q_t[:].rearrange("p j (h c) -> p (j h) c", c=HEAD_DIM)
+
+        def maximum_of_q(i):
+            q_max = work.tile([P, GROUPS], F32, name="q_max")
+            nc.vector.tensor_reduce(out=q_max[:], in_=tiles["q_t", i], axis=AXIS_X, op=ALU.max)
+            tiles["q_max", i] = q_max
+
+        def subtract_maximum_of_q(i):
+            q_exp = work.tile([P, GROUPS, HEAD_DIM], F32, name="q_exp")
+            nc.vector.tensor_tensor(out=q_exp[:], in0=tiles["q_t", i], in1=spread(tiles["q_max", i]), op=ALU.subtract)
+            tiles["q_exp", i] = q_exp
+
+        def exp_of_q(i):
+            nc.scalar.activation(out=tiles["q_exp", i][:], in_=tiles["q_exp", i][:], func=ACT.Exp)
+
+        def sum_of_q(i):
+            q_sum = work.tile([P, GROUPS], F32, name="q_sum")
+            nc.vector.tensor_reduce(out=q_sum[:], in_=tiles["q_exp", i][:], axis=AXIS_X, op=ALU.add)
+            tiles["q_sum", i] = q_sum
+
+        def invert_sum_of_q(i):
+            q_inv = work.tile([P, GROUPS], F32, name="q_inv")
+            nc.vector.reciprocal(out=q_inv[:], in_=tiles["q_sum", i][:])
+            tiles["q_inv", i] = q_inv
+
+        def normalise_q(i):
+            q_norm = work.tile([P, GROUPS, HEAD_DIM], F32, name="q_norm")
+            nc.vector.tensor_tensor(out=q_norm[:], in0=tiles["q_exp", i][:], in1=spread(tiles["q_inv", i]), op=ALU.mult)
+            tiles["q_norm", i] = q_norm
+
+        def transpose_q(i):
+            q_back = psum.tile([P, SUBTILES, P], F32, tag="q_back", name="q_back")
+            q_tiles = tiles["q_norm", i][:].rearrange("p (j h) c -> p j (h c)", h=HEADS)
             for j in range(SUBTILES):
                 nc.tensor.transpose(q_back[:, j, :], q_tiles[:, j, :], ident_f32[:])
-            q_out = loads.tile([P, CHUNK], F32)
-            nc.scalar.mul(out=q_out[:], in_=q_back[:].rearrange("p j n -> p (j n)"), mul=SCALE)
-            nc.sync.dma_start(out=q_soft_view[b, :, cols], in_=q_out[:])
+            tiles["q_back", i] = q_back
 
-            k_again = psum.tile([P, CHUNK], F32, tag="k_again")
-            channels_on_partitions(k_again, K_ROWS, b, t)
-            e_rows = work.tile([P, CHUNK], BF16)
+        def store_q(i):
+            q_out = loads.tile([P, CHUNK], F32, name="q_out")
+            nc.scalar.mul(out=q_out[:], in_=tiles["q_back", i][:].rearrange("p j n -> p (j n)"), mul=SCALE)
+            nc.sync.dma_start(out=q_soft_view[i // CHUNKS, :, columns(i)], in_=q_out[:])
+
+        def matmul_k_again(i):
+            k_again = psum.tile([P, CHUNK], F32, tag="k_again", name="k_again")
+            channels_on_partitions(k_again, K_ROWS, i)
+            tiles["k_again", i] = k_again
+
+        def exp_of_k(i):
+            b, t = i // CHUNKS, i % CHUNKS
+            if t == 0:
+                tiles["e_sums", b] = batch_pool.tile([P, CHUNKS], F32, name="e_sums")
+            e_rows = work.tile([P, CHUNK], BF16, name="e_rows")
             nc.scalar.activation(
                 out=e_rows[:],
-                in_=k_again[:],
+                in_=tiles["k_again", i][:],
                 func=ACT.Exp,
-                bias=state["minus_k_top"][:],
+                bias=tiles["minus_k_top", b][:],
                 scale=1.0,
-                accum_out=state["e_sums"][:, t : t + 1],
+                accum_out=tiles["e_sums", b][:, t : t + 1],
             )
-            e_t = psum.tile([P, SUBTILES, EMBED], BF16, tag="e_t")
+            tiles["e_rows", i] = e_rows
+
+        def transpose_e(i):
+            e_t = psum.tile([P, SUBTILES, EMBED], BF16, tag="e_t", name="e_t")
             for j in range(SUBTILES):
-                nc.tensor.transpose(e_t[:, j, :], e_rows[:, j * P : (j + 1) * P], ident_bf16[:])
-            e_grouped = work.tile([P, EMBED, PACK], BF16, align_bytes=64)
-            nc.scalar.copy(out=e_grouped[:], in_=e_t[:].rearrange("p j m -> p m j"))
-            e_codes = work.tile([P, EMBED], U32, align_bytes=64)
-            e_scales = work.tile([P, EMBED], U8, align_bytes=64)
+                nc.tensor.transpose(e_t[:, j, :], tiles["e_rows", i][:, j * P : (j + 1) * P], ident_bf16[:])
+            tiles["e_t", i] = e_t
+
+        def copy_out_e(i):
+            e_grouped = work.tile([P, EMBED, PACK], BF16, align_bytes=64, name="e_grouped")
+            nc.scalar.copy(out=e_grouped[:], in_=tiles["e_t", i][:].rearrange("p j m -> p m j"))
+            tiles["e_grouped", i] = e_grouped
+
+        def quantise_e(i):
+            e_codes = work.tile([P, EMBED], U32, align_bytes=64, name="e_codes")
+            e_scales = work.tile([P, EMBED], U8, align_bytes=64, name="e_scales")
             nc.vector.quantize_mx(
-                out=e_codes[:].bitcast(FP8X4), scales=e_scales[:], in_=e_grouped[:].rearrange("p m j -> p (m j)")
+                out=e_codes[:].bitcast(FP8X4),
+                scales=e_scales[:],
+                in_=tiles["e_grouped", i][:].rearrange("p m j -> p (m j)"),
             )
-            context = state["context"]
+            tiles["e_codes", i], tiles["e_scales", i] = e_codes, e_scales
+
+        def matmul_context(i):
+            b, t = i // CHUNKS, i % CHUNKS
+            if t == 0:
+                tiles["context", b] = psum.tile([P, EMBED], F32, tag="context", name="context")
             nc.tensor.matmul_mx(
-                out=context[:],
-                lhsT=e_codes[:].bitcast(FP8X4),
-                lhsT_scale=e_scales[:],
-                rhs=state["v_codes", b][:, t, :].bitcast(FP8X4),
-                rhs_scale=state["v_scales", b][:, t, :],
+                out=tiles["context", b][:],
+                lhsT=tiles["e_codes", i][:].bitcast(FP8X4),
+                lhsT_scale=tiles["e_scales", i][:],
+                rhs=tiles["v_codes", b][:, t, :].bitcast(FP8X4),
+                rhs_scale=tiles["v_scales", b][:, t, :],
                 start=(t == 0),
                 stop=(t == CHUNKS - 1),
             )
-            if t == CHUNKS - 1:
-                e_total = batch_pool.tile([P, 1], F32, name="e_total")
-                nc.vector.tensor_reduce(out=e_total[:], in_=state["e_sums"][:], axis=AXIS_X, op=ALU.add)
-                e_inv = batch_pool.tile([P, 1], F32, name="e_inv")
-                nc.vector.reciprocal(out=e_inv[:], in_=e_total[:])
-                context_out = batch_pool.tile([P, HEAD_DIM], F32, name="context_out")
-                for h in range(HEADS):
-                    rows = slice(h * HEAD_DIM, (h + 1) * HEAD_DIM)
-                    nc.vector.tensor_scalar_mul(
-                        out=context_out[rows, :], in0=context[rows, rows], scalar1=e_inv[rows, :]
-                    )
-                nc.sync.dma_start(out=context_view[b], in_=context_out[:])
 
-        steps = BATCH * CHUNKS
-        for step in range(steps + CHUNKS):
-            if step < steps:
-                first_pass(step // CHUNKS, step % CHUNKS)
-            if step >= CHUNKS:
-                second_pass((step - CHUNKS) // CHUNKS, (step - CHUNKS) % CHUNKS)
+        def store_context(i):
+            b = i // CHUNKS
+            if i % CHUNKS != CHUNKS - 1:
+                return
+            e_total = batch_pool.tile([P, 1], F32, name="e_total")
+            nc.vector.tensor_reduce(out=e_total[:], in_=tiles["e_sums", b][:], axis=AXIS_X, op=ALU.add)
+            e_inv = batch_pool.tile([P, 1], F32, name="e_inv")
+            nc.vector.reciprocal(out=e_inv[:], in_=e_total[:])
+            context_out = batch_pool.tile([P, HEAD_DIM], F32, name="context_out")
+            for h in range(HEADS):
+                rows = slice(h * HEAD_DIM, (h + 1) * HEAD_DIM)
+                nc.vector.tensor_scalar_mul(
+                    out=context_out[rows, :], in0=tiles["context", b][rows, rows], scalar1=e_inv[rows, :]
+                )
+            nc.sync.dma_start(out=context_view[b], in_=context_out[:])
+
+        def run(stage, i):
+            if 0 <= i < TOTAL:
+                stage(i)
+
+        for i in range(PREFETCH):
+            load_x(i)
+        for step in range(TOTAL + SECOND_PASS_LAG + 4):
+            a = step
+            c = step - SECOND_PASS_LAG
+            run(load_x, a + PREFETCH)
+            run(store_context, c - 4)
+            run(transpose_e, c - 1)
+            run(transpose_q, c - 2)
+            run(matmul_context, c - 3)
+            run(matmul_q, c + 1)
+            run(copy_out_v, a - 2)
+            run(copy_out_e, c - 1)
+            run(store_q, c - 2)
+            run(regroup_x_vector, a)
+            run(maximum_of_k, a - 2)
+            run(maximum_of_q, c)
+            run(quantise_x, a - 1)
+            run(subtract_maximum_of_q, c)
+            run(sum_of_q, c - 1)
+            run(quantise_v, a - 2)
+            run(invert_sum_of_q, c - 1)
+            run(quantise_e, c - 2)
+            run(normalise_q, c - 1)
+            run(matmul_k_first_and_v, a - 1)
+            run(matmul_k_again, c + 1)
+            run(exp_of_k, c)
+            run(regroup_x_scalar, a)
+            run(exp_of_q, c)

@@ -202,7 +202,7 @@ def tile_linearattention_pa_t_kernel(tc, xn, Wqkv, out_0, out_1):
 
         def normalise_q(i):
             q_norm = work.tile([P, GROUPS, HEAD_DIM], F32, name="q_norm")
-            nc.vector.tensor_tensor(out=q_norm[:], in0=tiles["q_exp", i][:], in1=spread(tiles["q_inv", i]), op=ALU.mult)
+            nc.gpsimd.tensor_tensor(out=q_norm[:], in0=tiles["q_exp", i][:], in1=spread(tiles["q_inv", i]), op=ALU.mult)
             tiles["q_norm", i] = q_norm
 
         def transpose_q(i):

@@ -26,14 +26,18 @@ CHUNK = 512
 CHUNKS = POSITIONS // CHUNK
 SUBTILES = CHUNK // P
 GROUPS = SUBTILES * HEADS
+HALVES = 2
+PAIR = HALVES * CHUNK
+PAIRS = POSITIONS // PAIR
 RUN = 4
 
 Q_ROWS, K_ROWS, V_ROWS = 0, 1, 2
 
-SECOND_PASS_LAG = CHUNKS + 2
-PREFETCH = 4
+SECOND_PASS_LAG = PAIRS + 1
+PREFETCH = 2
 
-VECTOR_COLS = 160
+VECTOR_COLS = 192
+GPSIMD_COLS = 512
 
 FLOPS = 2 * 3 * EMBED * CHANNELS * POSITIONS * BATCH + 2 * BATCH * HEADS * HEAD_DIM * HEAD_DIM * POSITIONS
 
@@ -46,8 +50,8 @@ def tile_linearattention_pa_t_kernel(tc, xn, Wqkv, out_0, out_1):
 
     with ExitStack() as stack:
         const = stack.enter_context(tc.tile_pool(name="const", bufs=1))
-        loads = stack.enter_context(tc.tile_pool(name="loads", bufs=6))
-        work = stack.enter_context(tc.tile_pool(name="work", bufs=4))
+        loads = stack.enter_context(tc.tile_pool(name="loads", bufs=4))
+        work = stack.enter_context(tc.tile_pool(name="work", bufs=3))
         batch_pool = stack.enter_context(tc.tile_pool(name="batch", bufs=2))
         psum = stack.enter_context(tc.psum_pool(name="psum", bufs=1))
         stack.enter_context(tc.manual_schedule())
@@ -73,30 +77,31 @@ def tile_linearattention_pa_t_kernel(tc, xn, Wqkv, out_0, out_1):
                 in_=w_grouped[:, r].rearrange("p m t -> p (m t)"),
             )
 
-        TOTAL = BATCH * CHUNKS
+        TOTAL = BATCH * PAIRS
         tiles = {}
 
-        def columns(i):
-            return slice((i % CHUNKS) * CHUNK, (i % CHUNKS + 1) * CHUNK)
+        def chunk_of(i, u):
+            return (i % PAIRS) * HALVES + u
 
-        def channels_on_partitions(bank, rows, i):
+        def channels_on_partitions(bank, rows, i, u):
+            first = chunk_of(i, u) * CHUNK
             nc.tensor.matmul_mx(
                 out=bank[:],
                 lhsT=w_codes[:, rows, :].bitcast(FP8X4),
                 lhsT_scale=w_scales[:, rows, :],
-                rhs=tiles["x_codes", i // CHUNKS][:, columns(i)].bitcast(FP8X4),
-                rhs_scale=tiles["x_scales", i // CHUNKS][:, columns(i)],
+                rhs=tiles["x_codes", i // PAIRS][:, first : first + CHUNK].bitcast(FP8X4),
+                rhs_scale=tiles["x_scales", i // PAIRS][:, first : first + CHUNK],
                 start=True,
                 stop=True,
             )
 
-        def positions_on_partitions(bank, rows, i):
+        def positions_on_partitions(bank, rows, i, u):
             for j in range(SUBTILES):
-                first = (i % CHUNKS) * CHUNK + j * P
+                first = chunk_of(i, u) * CHUNK + j * P
                 nc.tensor.matmul_mx(
                     out=bank[:, j, :],
-                    lhsT=tiles["x_codes", i // CHUNKS][:, first : first + P].bitcast(FP8X4),
-                    lhsT_scale=tiles["x_scales", i // CHUNKS][:, first : first + P],
+                    lhsT=tiles["x_codes", i // PAIRS][:, first : first + P].bitcast(FP8X4),
+                    lhsT_scale=tiles["x_scales", i // PAIRS][:, first : first + P],
                     rhs=w_codes[:, rows, :].bitcast(FP8X4),
                     rhs_scale=w_scales[:, rows, :],
                     start=True,
@@ -104,50 +109,62 @@ def tile_linearattention_pa_t_kernel(tc, xn, Wqkv, out_0, out_1):
                 )
 
         def load_x(i):
-            x_raw = loads.tile([P, PACK, CHUNK], BF16, name="x_raw")
-            nc.sync.dma_start(out=x_raw[:], in_=xn_view[i // CHUNKS, :, :, columns(i)])
+            first = (i % PAIRS) * PAIR
+            x_raw = loads.tile([P, PACK, PAIR], BF16, name="x_raw")
+            nc.sync.dma_start(out=x_raw[:], in_=xn_view[i // PAIRS, :, :, first : first + PAIR])
             tiles["x_raw", i] = x_raw
 
-        def regroup_x_vector(i):
-            x_grouped = work.tile([P, CHUNK, PACK], BF16, align_bytes=64, name="x_grouped")
+        def regroup_x_gpsimd(i):
+            x_grouped = work.tile([P, PAIR, PACK], BF16, align_bytes=64, name="x_grouped", bufs=2)
             tiles["x_grouped", i] = x_grouped
+            share = slice(VECTOR_COLS, VECTOR_COLS + GPSIMD_COLS)
+            nc.gpsimd.tensor_scalar(
+                out=x_grouped[:, share, :],
+                in0=tiles["x_raw", i][:, :, share].rearrange("p t n -> p n t"),
+                scalar1=1.0,
+                scalar2=0.0,
+                op0=ALU.mult,
+                op1=ALU.add,
+            )
+
+        def regroup_x_vector(i):
+            share = slice(0, VECTOR_COLS)
             nc.vector.tensor_copy(
-                out=x_grouped[:, :VECTOR_COLS, :].rearrange("p (n i) t -> p n t i", i=RUN),
-                in_=tiles["x_raw", i][:, :, :VECTOR_COLS].rearrange("p t (n i) -> p n t i", i=RUN),
+                out=tiles["x_grouped", i][:, share, :].rearrange("p (n i) t -> p n t i", i=RUN),
+                in_=tiles["x_raw", i][:, :, share].rearrange("p t (n i) -> p n t i", i=RUN),
             )
 
         def regroup_x_scalar(i):
+            share = slice(VECTOR_COLS + GPSIMD_COLS, PAIR)
             nc.scalar.copy(
-                out=tiles["x_grouped", i][:, VECTOR_COLS:, :].rearrange("p (n i) t -> p n t i", i=RUN),
-                in_=tiles["x_raw", i][:, :, VECTOR_COLS:].rearrange("p t (n i) -> p n t i", i=RUN),
+                out=tiles["x_grouped", i][:, share, :].rearrange("p (n i) t -> p n t i", i=RUN),
+                in_=tiles["x_raw", i][:, :, share].rearrange("p t (n i) -> p n t i", i=RUN),
             )
 
         def quantise_x(i):
-            b = i // CHUNKS
-            if i % CHUNKS == 0:
+            b = i // PAIRS
+            if i % PAIRS == 0:
                 tiles["x_codes", b] = batch_pool.tile([P, POSITIONS], U32, align_bytes=64, name="x_codes")
                 tiles["x_scales", b] = batch_pool.tile([P, POSITIONS], U8, align_bytes=64, name="x_scales")
-                tiles["v_codes", b] = batch_pool.tile([P, CHUNKS, EMBED], U32, align_bytes=64, name="v_codes", bufs=3)
-                tiles["v_scales", b] = batch_pool.tile([P, CHUNKS, EMBED], U8, align_bytes=64, name="v_scales", bufs=3)
+                tiles["v_codes", b] = batch_pool.tile([P, CHUNKS * EMBED], U32, align_bytes=64, name="v_codes", bufs=3)
+                tiles["v_scales", b] = batch_pool.tile([P, CHUNKS * EMBED], U8, align_bytes=64, name="v_scales", bufs=3)
                 tiles["k_max", b] = batch_pool.tile([P, CHUNKS], F32, name="k_max")
+            first = (i % PAIRS) * PAIR
             nc.vector.quantize_mx(
-                out=tiles["x_codes", b][:, columns(i)].bitcast(FP8X4),
-                scales=tiles["x_scales", b][:, columns(i)],
+                out=tiles["x_codes", b][:, first : first + PAIR].bitcast(FP8X4),
+                scales=tiles["x_scales", b][:, first : first + PAIR],
                 in_=tiles["x_grouped", i][:].rearrange("p n t -> p (n t)"),
             )
 
-        def matmul_k_first_and_v(i):
+        def matmul_k_first(i, u):
             k_first = psum.tile([P, CHUNK], F32, tag="k_first", name="k_first")
-            channels_on_partitions(k_first, K_ROWS, i)
-            tiles["k_first", i] = k_first
-            v_t = psum.tile([P, SUBTILES, EMBED], F32, tag="v_t", name="v_t")
-            positions_on_partitions(v_t, V_ROWS, i)
-            tiles["v_t", i] = v_t
+            channels_on_partitions(k_first, K_ROWS, i, u)
+            tiles["k_first", i, u] = k_first
 
-        def maximum_of_k(i):
-            b, t = i // CHUNKS, i % CHUNKS
+        def maximum_of_k(i, u):
+            b, t = i // PAIRS, chunk_of(i, u)
             nc.vector.tensor_reduce(
-                out=tiles["k_max", b][:, t : t + 1], in_=tiles["k_first", i][:], axis=AXIS_X, op=ALU.max
+                out=tiles["k_max", b][:, t : t + 1], in_=tiles["k_first", i, u][:], axis=AXIS_X, op=ALU.max
             )
             if t == CHUNKS - 1:
                 k_top = batch_pool.tile([P, 1], F32, name="k_top")
@@ -156,125 +173,151 @@ def tile_linearattention_pa_t_kernel(tc, xn, Wqkv, out_0, out_1):
                 nc.vector.tensor_scalar_mul(out=minus_k_top[:], in0=k_top[:], scalar1=-1.0)
                 tiles["minus_k_top", b] = minus_k_top
 
-        def copy_out_v(i):
-            v_grouped = work.tile([P, EMBED, PACK], BF16, align_bytes=64, name="v_grouped")
-            nc.scalar.copy(out=v_grouped[:], in_=tiles["v_t", i][:].rearrange("p j m -> p m j"))
-            tiles["v_grouped", i] = v_grouped
+        def matmul_v(i, u):
+            v_t = psum.tile([P, SUBTILES, EMBED], F32, tag="v_t", name="v_t")
+            positions_on_partitions(v_t, V_ROWS, i, u)
+            tiles["v_t", i, u] = v_t
+
+        def copy_out_v(i, u):
+            if u == 0:
+                tiles["v_grouped", i] = work.tile([P, HALVES, EMBED, PACK], BF16, align_bytes=64, name="v_grouped")
+            nc.scalar.copy(out=tiles["v_grouped", i][:, u], in_=tiles["v_t", i, u][:].rearrange("p j m -> p m j"))
 
         def quantise_v(i):
-            b, t = i // CHUNKS, i % CHUNKS
+            b = i // PAIRS
+            first = chunk_of(i, 0) * EMBED
             nc.vector.quantize_mx(
-                out=tiles["v_codes", b][:, t, :].bitcast(FP8X4),
-                scales=tiles["v_scales", b][:, t, :],
-                in_=tiles["v_grouped", i][:].rearrange("p m j -> p (m j)"),
+                out=tiles["v_codes", b][:, first : first + HALVES * EMBED].bitcast(FP8X4),
+                scales=tiles["v_scales", b][:, first : first + HALVES * EMBED],
+                in_=tiles["v_grouped", i][:].rearrange("p u m j -> p (u m j)"),
             )
 
         def spread(per_group):
-            return per_group[:].unsqueeze(2).to_broadcast([P, GROUPS, HEAD_DIM])
+            return per_group.unsqueeze(2).to_broadcast([P, per_group.shape[1], HEAD_DIM])
 
-        def matmul_q(i):
+        def matmul_q(i, u):
             q_t = psum.tile([P, SUBTILES, EMBED], F32, tag="q_t", bufs=2, name="q_t")
-            positions_on_partitions(q_t, Q_ROWS, i)
-            tiles["q_t", i] = q_t[:].rearrange("p j (h c) -> p (j h) c", c=HEAD_DIM)
+            positions_on_partitions(q_t, Q_ROWS, i, u)
+            tiles["q_t", i, u] = q_t[:].rearrange("p j (h c) -> p (j h) c", c=HEAD_DIM)
 
-        def maximum_of_q(i):
-            q_max = work.tile([P, GROUPS], F32, name="q_max")
-            nc.vector.tensor_reduce(out=q_max[:], in_=tiles["q_t", i], axis=AXIS_X, op=ALU.max)
-            tiles["q_max", i] = q_max
+        def maximum_of_q(i, u):
+            if u == 0:
+                tiles["q_max", i] = work.tile([P, HALVES, GROUPS], F32, name="q_max")
+            nc.vector.tensor_reduce(out=tiles["q_max", i][:, u, :], in_=tiles["q_t", i, u], axis=AXIS_X, op=ALU.max)
 
-        def subtract_maximum_of_q(i):
-            q_exp = work.tile([P, GROUPS, HEAD_DIM], F32, name="q_exp")
-            nc.vector.tensor_tensor(out=q_exp[:], in0=tiles["q_t", i], in1=spread(tiles["q_max", i]), op=ALU.subtract)
-            tiles["q_exp", i] = q_exp
+        def subtract_maximum_of_q(i, u):
+            if u == 0:
+                tiles["q_exp", i] = work.tile([P, HALVES, GROUPS, HEAD_DIM], F32, name="q_exp")
+            nc.vector.tensor_tensor(
+                out=tiles["q_exp", i][:, u],
+                in0=tiles["q_t", i, u],
+                in1=spread(tiles["q_max", i][:, u, :]),
+                op=ALU.subtract,
+            )
 
         def exp_of_q(i):
             nc.scalar.activation(out=tiles["q_exp", i][:], in_=tiles["q_exp", i][:], func=ACT.Exp)
 
         def sum_of_q(i):
-            q_sum = work.tile([P, GROUPS], F32, name="q_sum")
-            nc.vector.tensor_reduce(out=q_sum[:], in_=tiles["q_exp", i][:], axis=AXIS_X, op=ALU.add)
+            q_sum = work.tile([P, HALVES * GROUPS], F32, name="q_sum")
+            nc.vector.tensor_reduce(
+                out=q_sum[:], in_=tiles["q_exp", i][:].rearrange("p u g c -> p (u g) c"), axis=AXIS_X, op=ALU.add
+            )
             tiles["q_sum", i] = q_sum
 
         def invert_sum_of_q(i):
-            q_inv = work.tile([P, GROUPS], F32, name="q_inv")
+            q_inv = work.tile([P, HALVES * GROUPS], F32, name="q_inv")
             nc.vector.reciprocal(out=q_inv[:], in_=tiles["q_sum", i][:])
             tiles["q_inv", i] = q_inv
 
         def normalise_q(i):
-            q_norm = work.tile([P, GROUPS, HEAD_DIM], F32, name="q_norm")
-            nc.gpsimd.tensor_tensor(out=q_norm[:], in0=tiles["q_exp", i][:], in1=spread(tiles["q_inv", i]), op=ALU.mult)
+            q_norm = work.tile([P, HALVES * GROUPS, HEAD_DIM], F32, name="q_norm")
+            nc.gpsimd.tensor_tensor(
+                out=q_norm[:],
+                in0=tiles["q_exp", i][:].rearrange("p u g c -> p (u g) c"),
+                in1=spread(tiles["q_inv", i][:]),
+                op=ALU.mult,
+            )
             tiles["q_norm", i] = q_norm
 
-        def transpose_q(i):
+        def transpose_q(i, u):
             q_back = psum.tile([P, SUBTILES, P], F32, tag="q_back", name="q_back")
-            q_tiles = tiles["q_norm", i][:].rearrange("p (j h) c -> p j (h c)", h=HEADS)
+            q_tiles = tiles["q_norm", i][:].rearrange("p (u j h) c -> p u j (h c)", u=HALVES, h=HEADS)
             for j in range(SUBTILES):
-                nc.tensor.transpose(q_back[:, j, :], q_tiles[:, j, :], ident_f32[:])
-            tiles["q_back", i] = q_back
+                nc.tensor.transpose(q_back[:, j, :], q_tiles[:, u, j, :], ident_f32[:])
+            tiles["q_back", i, u] = q_back
 
-        def store_q(i):
-            q_out = loads.tile([P, CHUNK], F32, name="q_out")
-            nc.scalar.mul(out=q_out[:], in_=tiles["q_back", i][:].rearrange("p j n -> p (j n)"), mul=SCALE)
-            nc.sync.dma_start(out=q_soft_view[i // CHUNKS, :, columns(i)], in_=q_out[:])
+        def copy_out_q(i, u):
+            if u == 0:
+                tiles["q_out", i] = loads.tile([P, HALVES, CHUNK], F32, name="q_out")
+            q_out = tiles["q_out", i]
+            nc.scalar.mul(out=q_out[:, u, :], in_=tiles["q_back", i, u][:].rearrange("p j n -> p (j n)"), mul=SCALE)
+            if u == HALVES - 1:
+                first = (i % PAIRS) * PAIR
+                nc.sync.dma_start(
+                    out=q_soft_view[i // PAIRS, :, first : first + PAIR], in_=q_out[:].rearrange("p u n -> p (u n)")
+                )
 
-        def matmul_k_again(i):
+        def matmul_k_again(i, u):
             k_again = psum.tile([P, CHUNK], F32, tag="k_again", name="k_again")
-            channels_on_partitions(k_again, K_ROWS, i)
-            tiles["k_again", i] = k_again
+            channels_on_partitions(k_again, K_ROWS, i, u)
+            tiles["k_again", i, u] = k_again
 
-        def exp_of_k(i):
-            b, t = i // CHUNKS, i % CHUNKS
+        def exp_of_k(i, u):
+            b, t = i // PAIRS, chunk_of(i, u)
             if t == 0:
                 tiles["e_sums", b] = batch_pool.tile([P, CHUNKS], F32, name="e_sums")
-            e_rows = work.tile([P, CHUNK], BF16, name="e_rows")
+            if u == 0:
+                tiles["e_rows", i] = work.tile([P, HALVES * SUBTILES, P], BF16, name="e_rows")
             nc.scalar.activation(
-                out=e_rows[:],
-                in_=tiles["k_again", i][:],
+                out=tiles["e_rows", i][:, u * SUBTILES : (u + 1) * SUBTILES, :].rearrange("p j n -> p (j n)"),
+                in_=tiles["k_again", i, u][:],
                 func=ACT.Exp,
                 bias=tiles["minus_k_top", b][:],
                 scale=1.0,
                 accum_out=tiles["e_sums", b][:, t : t + 1],
             )
-            tiles["e_rows", i] = e_rows
 
         def transpose_e(i):
-            e_t = psum.tile([P, SUBTILES, EMBED], BF16, tag="e_t", name="e_t")
-            for j in range(SUBTILES):
-                nc.tensor.transpose(e_t[:, j, :], tiles["e_rows", i][:, j * P : (j + 1) * P], ident_bf16[:])
+            e_t = psum.tile([P, HALVES * SUBTILES, EMBED], BF16, tag="e_t", name="e_t")
+            for j in range(HALVES * SUBTILES):
+                nc.tensor.transpose(e_t[:, j, :], tiles["e_rows", i][:, j, :], ident_bf16[:])
             tiles["e_t", i] = e_t
 
         def copy_out_e(i):
-            e_grouped = work.tile([P, EMBED, PACK], BF16, align_bytes=64, name="e_grouped")
-            nc.scalar.copy(out=e_grouped[:], in_=tiles["e_t", i][:].rearrange("p j m -> p m j"))
+            e_grouped = work.tile([P, HALVES, EMBED, PACK], BF16, align_bytes=64, name="e_grouped")
+            nc.scalar.copy(out=e_grouped[:], in_=tiles["e_t", i][:].rearrange("p (u j) m -> p u m j", u=HALVES))
             tiles["e_grouped", i] = e_grouped
 
         def quantise_e(i):
-            e_codes = work.tile([P, EMBED], U32, align_bytes=64, name="e_codes")
-            e_scales = work.tile([P, EMBED], U8, align_bytes=64, name="e_scales")
+            e_codes = work.tile([P, HALVES, EMBED], U32, align_bytes=64, name="e_codes")
+            e_scales = work.tile([P, HALVES, EMBED], U8, align_bytes=64, name="e_scales")
             nc.vector.quantize_mx(
-                out=e_codes[:].bitcast(FP8X4),
-                scales=e_scales[:],
-                in_=tiles["e_grouped", i][:].rearrange("p m j -> p (m j)"),
+                out=e_codes[:].rearrange("p u m -> p (u m)").bitcast(FP8X4),
+                scales=e_scales[:].rearrange("p u m -> p (u m)"),
+                in_=tiles["e_grouped", i][:].rearrange("p u m j -> p (u m j)"),
             )
             tiles["e_codes", i], tiles["e_scales", i] = e_codes, e_scales
 
         def matmul_context(i):
-            b, t = i // CHUNKS, i % CHUNKS
-            if t == 0:
+            b = i // PAIRS
+            if i % PAIRS == 0:
                 tiles["context", b] = psum.tile([P, EMBED], F32, tag="context", name="context")
-            nc.tensor.matmul_mx(
-                out=tiles["context", b][:],
-                lhsT=tiles["e_codes", i][:].bitcast(FP8X4),
-                lhsT_scale=tiles["e_scales", i][:],
-                rhs=tiles["v_codes", b][:, t, :].bitcast(FP8X4),
-                rhs_scale=tiles["v_scales", b][:, t, :],
-                start=(t == 0),
-                stop=(t == CHUNKS - 1),
-            )
+            for u in range(HALVES):
+                t = chunk_of(i, u)
+                nc.tensor.matmul_mx(
+                    out=tiles["context", b][:],
+                    lhsT=tiles["e_codes", i][:, u, :].bitcast(FP8X4),
+                    lhsT_scale=tiles["e_scales", i][:, u, :],
+                    rhs=tiles["v_codes", b][:, t * EMBED : (t + 1) * EMBED].bitcast(FP8X4),
+                    rhs_scale=tiles["v_scales", b][:, t * EMBED : (t + 1) * EMBED],
+                    start=(t == 0),
+                    stop=(t == CHUNKS - 1),
+                )
 
         def store_context(i):
-            b = i // CHUNKS
-            if i % CHUNKS != CHUNKS - 1:
+            b = i // PAIRS
+            if i % PAIRS != PAIRS - 1:
                 return
             e_total = batch_pool.tile([P, 1], F32, name="e_total")
             nc.vector.tensor_reduce(out=e_total[:], in_=tiles["e_sums", b][:], axis=AXIS_X, op=ALU.add)
@@ -288,36 +331,50 @@ def tile_linearattention_pa_t_kernel(tc, xn, Wqkv, out_0, out_1):
                 )
             nc.sync.dma_start(out=context_view[b], in_=context_out[:])
 
-        def run(stage, i):
+        def run(stage, i, *half):
             if 0 <= i < TOTAL:
-                stage(i)
+                stage(i, *half)
 
         for i in range(PREFETCH):
             load_x(i)
         for step in range(TOTAL + SECOND_PASS_LAG + 4):
-            a = step
-            c = step - SECOND_PASS_LAG
-            run(load_x, a + PREFETCH)
-            run(store_context, c - 4)
-            run(transpose_e, c - 1)
-            run(transpose_q, c - 2)
-            run(matmul_context, c - 3)
-            run(matmul_q, c + 1)
-            run(copy_out_v, a - 2)
-            run(copy_out_e, c - 1)
-            run(store_q, c - 2)
-            run(regroup_x_vector, a)
-            run(maximum_of_k, a - 2)
-            run(maximum_of_q, c)
-            run(quantise_x, a - 1)
-            run(subtract_maximum_of_q, c)
+            r = step
+            a = step - 1
+            c = a - SECOND_PASS_LAG
+            run(load_x, r + PREFETCH)
+            run(regroup_x_gpsimd, r)
+            run(matmul_context, c - 2)
+            run(copy_out_v, a - 1, 0)
+            run(matmul_v, a - 1, 1)
+            run(exp_of_k, c, 0)
+            run(matmul_k_again, c, 1)
+            run(maximum_of_q, c, 0)
             run(sum_of_q, c - 1)
-            run(quantise_v, a - 2)
+            run(maximum_of_k, a - 1, 0)
+            run(matmul_k_first, a - 1, 1)
             run(invert_sum_of_q, c - 1)
-            run(quantise_e, c - 2)
             run(normalise_q, c - 1)
-            run(matmul_k_first_and_v, a - 1)
-            run(matmul_k_again, c + 1)
-            run(exp_of_k, c)
-            run(regroup_x_scalar, a)
+            run(subtract_maximum_of_q, c, 0)
+            run(matmul_q, c + 1, 0)
+            run(copy_out_q, c - 2, 0)
+            run(transpose_q, c - 2, 1)
+            run(copy_out_e, c - 1)
+            run(copy_out_v, a - 1, 1)
+            run(exp_of_k, c, 1)
+            run(transpose_e, c)
+            run(copy_out_q, c - 2, 1)
+            run(transpose_q, c - 1, 0)
+            run(matmul_k_again, c + 1, 0)
+            run(maximum_of_q, c, 1)
+            run(maximum_of_k, a - 1, 1)
+            run(subtract_maximum_of_q, c, 1)
+            run(matmul_q, c + 1, 1)
+            run(quantise_x, a)
+            run(matmul_k_first, a, 0)
+            run(matmul_v, a, 0)
+            run(quantise_v, a - 1)
+            run(regroup_x_vector, r)
+            run(quantise_e, c - 1)
+            run(store_context, c - 2)
+            run(regroup_x_scalar, r)
             run(exp_of_q, c)

@@ -29,6 +29,7 @@ GROUPS = SUBTILES * HEADS
 HALVES = 2
 PAIR = HALVES * CHUNK
 PAIRS = POSITIONS // PAIR
+WORDS = SUBTILES // 2
 RUN = 4
 
 Q_ROWS, K_ROWS, V_ROWS = 0, 1, 2
@@ -268,10 +269,10 @@ def tile_linearattention_pa_t_kernel(tc, xn, Wqkv, out_0, out_1):
             if t == 0:
                 tiles["e_sums", b] = batch_pool.tile([P, CHUNKS], F32, name="e_sums")
             if u == 0:
-                tiles["e_rows", i] = work.tile([P, HALVES * SUBTILES, P], BF16, name="e_rows")
+                tiles["e_rows", i] = work.tile([P, HALVES, WORDS, P, 2], BF16, name="e_rows")
             nc.scalar.activation(
-                out=tiles["e_rows", i][:, u * SUBTILES : (u + 1) * SUBTILES, :].rearrange("p j n -> p (j n)"),
-                in_=tiles["k_again", i, u][:],
+                out=tiles["e_rows", i][:, u],
+                in_=tiles["k_again", i, u][:].rearrange("p (w i n) -> p w n i", w=WORDS, i=2),
                 func=ACT.Exp,
                 bias=tiles["minus_k_top", b][:],
                 scale=1.0,
@@ -279,14 +280,18 @@ def tile_linearattention_pa_t_kernel(tc, xn, Wqkv, out_0, out_1):
             )
 
         def transpose_e(i):
-            e_t = psum.tile([P, HALVES * SUBTILES, EMBED], BF16, tag="e_t", name="e_t")
-            for j in range(HALVES * SUBTILES):
-                nc.tensor.transpose(e_t[:, j, :], tiles["e_rows", i][:, j, :], ident_bf16[:])
+            e_words = tiles["e_rows", i][:].rearrange("p u w n i -> p (u w n i)").bitcast(F32)
+            e_t = psum.tile([P, HALVES * WORDS, EMBED], F32, tag="e_t", name="e_t")
+            for w in range(HALVES * WORDS):
+                nc.tensor.transpose(e_t[:, w, :], e_words[:, w * P : (w + 1) * P], ident_f32[:])
             tiles["e_t", i] = e_t
 
         def copy_out_e(i):
             e_grouped = work.tile([P, HALVES, EMBED, PACK], BF16, align_bytes=64, name="e_grouped")
-            nc.scalar.copy(out=e_grouped[:], in_=tiles["e_t", i][:].rearrange("p (u j) m -> p u m j", u=HALVES))
+            nc.scalar.copy(
+                out=e_grouped[:].rearrange("p u m j -> p (u m j)").bitcast(F32).rearrange("p (u m w) -> p u m w", u=HALVES, w=WORDS),
+                in_=tiles["e_t", i][:].rearrange("p (u w) m -> p u m w", u=HALVES),
+            )
             tiles["e_grouped", i] = e_grouped
 
         def quantise_e(i):

@@ -38,7 +38,7 @@ SECOND_PASS_LAG = PAIRS + 1
 PREFETCH = 2
 
 VECTOR_COLS = 192
-GPSIMD_COLS = 512
+GPSIMD_COLS = 448
 
 FLOPS = 2 * 3 * EMBED * CHANNELS * POSITIONS * BATCH + 2 * BATCH * HEADS * HEAD_DIM * HEAD_DIM * POSITIONS
 
@@ -116,7 +116,7 @@ def tile_linearattention_pa_t_kernel(tc, xn, Wqkv, out_0, out_1):
             tiles["x_raw", i] = x_raw
 
         def regroup_x_gpsimd(i):
-            x_grouped = work.tile([P, PAIR, PACK], BF16, align_bytes=64, name="x_grouped", bufs=2)
+            x_grouped = work.tile([P, PAIR, PACK], BF16, align_bytes=64, name="x_grouped", bufs=1)
             tiles["x_grouped", i] = x_grouped
             share = slice(VECTOR_COLS, VECTOR_COLS + GPSIMD_COLS)
             nc.gpsimd.tensor_scalar(
@@ -208,7 +208,7 @@ def tile_linearattention_pa_t_kernel(tc, xn, Wqkv, out_0, out_1):
 
         def subtract_maximum_of_q(i, u):
             if u == 0:
-                tiles["q_exp", i] = work.tile([P, HALVES, GROUPS, HEAD_DIM], F32, name="q_exp")
+                tiles["q_exp", i] = work.tile([P, HALVES, GROUPS, HEAD_DIM], F32, name="q_exp", bufs=4)
             nc.vector.tensor_tensor(
                 out=tiles["q_exp", i][:, u],
                 in0=tiles["q_t", i, u],
@@ -342,44 +342,45 @@ def tile_linearattention_pa_t_kernel(tc, xn, Wqkv, out_0, out_1):
 
         for i in range(PREFETCH):
             load_x(i)
-        for step in range(TOTAL + SECOND_PASS_LAG + 4):
+        for step in range(TOTAL + 5 + 5):
             r = step
             a = step - 1
-            c = a - SECOND_PASS_LAG
+            q = a - 1
+            c = a - 5
             run(load_x, r + PREFETCH)
+            run(quantise_v, a - 2)
+            run(quantise_e, c - 2)
+            run(quantise_x, a)
             run(regroup_x_gpsimd, r)
+            run(regroup_x_vector, r)
+            run(normalise_q, q - 2)
             run(matmul_context, c - 2)
-            run(copy_out_v, a - 1, 0)
-            run(matmul_v, a - 1, 1)
+            run(exp_of_q, q - 1)
             run(exp_of_k, c, 0)
             run(matmul_k_again, c, 1)
-            run(maximum_of_q, c, 0)
-            run(sum_of_q, c - 1)
+            run(maximum_of_q, q, 0)
             run(maximum_of_k, a - 1, 0)
             run(matmul_k_first, a - 1, 1)
-            run(invert_sum_of_q, c - 1)
-            run(normalise_q, c - 1)
-            run(subtract_maximum_of_q, c, 0)
-            run(matmul_q, c + 1, 0)
-            run(copy_out_q, c - 2, 0)
-            run(transpose_q, c - 2, 1)
-            run(copy_out_e, c - 1)
-            run(copy_out_v, a - 1, 1)
+            run(copy_out_v, a - 1, 0)
+            run(regroup_x_scalar, r)
+            run(matmul_v, a - 1, 1)
+            run(sum_of_q, q - 1)
+            run(subtract_maximum_of_q, q, 0)
+            run(matmul_q, q + 1, 0)
+            run(copy_out_q, q - 3, 0)
+            run(transpose_q, q - 3, 1)
             run(exp_of_k, c, 1)
             run(transpose_e, c)
-            run(copy_out_q, c - 2, 1)
-            run(transpose_q, c - 1, 0)
             run(matmul_k_again, c + 1, 0)
-            run(maximum_of_q, c, 1)
+            run(invert_sum_of_q, q - 1)
+            run(maximum_of_q, q, 1)
             run(maximum_of_k, a - 1, 1)
-            run(subtract_maximum_of_q, c, 1)
-            run(matmul_q, c + 1, 1)
-            run(quantise_x, a)
             run(matmul_k_first, a, 0)
+            run(copy_out_v, a - 1, 1)
             run(matmul_v, a, 0)
-            run(quantise_v, a - 1)
-            run(regroup_x_vector, r)
-            run(quantise_e, c - 1)
+            run(subtract_maximum_of_q, q, 1)
+            run(matmul_q, q + 1, 1)
+            run(copy_out_q, q - 3, 1)
+            run(copy_out_e, c)
+            run(transpose_q, q - 2, 0)
             run(store_context, c - 2)
-            run(regroup_x_scalar, r)
-            run(exp_of_q, c)

@@ -37,8 +37,8 @@ Q_ROWS, K_ROWS, V_ROWS = 0, 1, 2
 SECOND_PASS_LAG = PAIRS + 1
 PREFETCH = 2
 
-VECTOR_COLS = 192
-GPSIMD_COLS = 448
+VECTOR_COLS = 64
+GPSIMD_COLS = 544
 
 FLOPS = 2 * 3 * EMBED * CHANNELS * POSITIONS * BATCH + 2 * BATCH * HEADS * HEAD_DIM * HEAD_DIM * POSITIONS
 

@@ -38,7 +38,7 @@ SECOND_PASS_LAG = PAIRS + 1
 PREFETCH = 2
 
 VECTOR_COLS = 64
-GPSIMD_COLS = 544
+GPSIMD_COLS = 448
 
 FLOPS = 2 * 3 * EMBED * CHANNELS * POSITIONS * BATCH + 2 * BATCH * HEADS * HEAD_DIM * HEAD_DIM * POSITIONS
 
@@ -63,21 +63,11 @@ def tile_linearattention_pa_t_kernel(tc, xn, Wqkv, out_0, out_1):
         make_identity(nc, ident_f32[:])
 
         w_rows = const.tile([P, 3, CHANNELS], BF16)
-        nc.sync.dma_start(out=w_rows[:], in_=Wqkv.rearrange("(r p) c -> p r c", p=P))
         w_grouped = const.tile([P, 3, EMBED, PACK], BF16, align_bytes=64)
         w_codes = const.tile([P, 3, EMBED], U32, align_bytes=64)
         w_scales = const.tile([P, 3, EMBED], U8, align_bytes=64)
-        for r in range(3):
-            w_t = psum.tile([P, PACK, P], BF16, tag="e_t")
-            for t in range(PACK):
-                nc.tensor.transpose(w_t[:, t, :], w_rows[:, r, t * P : (t + 1) * P], ident_bf16[:])
-            nc.vector.tensor_copy(out=w_grouped[:, r], in_=w_t[:].rearrange("p t m -> p m t"))
-            nc.vector.quantize_mx(
-                out=w_codes[:, r, :].bitcast(FP8X4),
-                scales=w_scales[:, r, :],
-                in_=w_grouped[:, r].rearrange("p m t -> p (m t)"),
-            )
-
+        LAST = (BATCH - 1) * PAIRS
+        LAST_BANKS = (("k_again", "k_first"), ("v_t", "q_t"))
         TOTAL = BATCH * PAIRS
         tiles = {}
 
@@ -115,10 +105,28 @@ def tile_linearattention_pa_t_kernel(tc, xn, Wqkv, out_0, out_1):
             nc.sync.dma_start(out=x_raw[:], in_=xn_view[i // PAIRS, :, :, first : first + PAIR])
             tiles["x_raw", i] = x_raw
 
+        def shares(i):
+            return (448, 320) if i < 2 else (VECTOR_COLS, GPSIMD_COLS)
+
+        def regroup_w():
+            for r in range(3):
+                w_t = psum.tile([P, PACK, P], BF16, tag=("e_t", "k_first", "v_t")[r], name="w_t")
+                for t in range(PACK):
+                    nc.tensor.transpose(w_t[:, t, :], w_rows[:, r, t * P : (t + 1) * P], ident_bf16[:])
+                nc.scalar.copy(out=w_grouped[:, r], in_=w_t[:].rearrange("p t m -> p m t"))
+
+        def quantise_w():
+            for r in range(3):
+                nc.vector.quantize_mx(
+                    out=w_codes[:, r, :].bitcast(FP8X4),
+                    scales=w_scales[:, r, :],
+                    in_=w_grouped[:, r].rearrange("p m t -> p (m t)"),
+                )
+
         def regroup_x_gpsimd(i):
             x_grouped = work.tile([P, PAIR, PACK], BF16, align_bytes=64, name="x_grouped", bufs=1)
             tiles["x_grouped", i] = x_grouped
-            share = slice(VECTOR_COLS, VECTOR_COLS + GPSIMD_COLS)
+            share = slice(shares(i)[0], sum(shares(i)))
             nc.gpsimd.tensor_scalar(
                 out=x_grouped[:, share, :],
                 in0=tiles["x_raw", i][:, :, share].rearrange("p t n -> p n t"),
@@ -129,14 +137,14 @@ def tile_linearattention_pa_t_kernel(tc, xn, Wqkv, out_0, out_1):
             )
 
         def regroup_x_vector(i):
-            share = slice(0, VECTOR_COLS)
+            share = slice(0, shares(i)[0])
             nc.vector.tensor_copy(
                 out=tiles["x_grouped", i][:, share, :].rearrange("p (n i) t -> p n t i", i=RUN),
                 in_=tiles["x_raw", i][:, :, share].rearrange("p t (n i) -> p n t i", i=RUN),
             )
 
         def regroup_x_scalar(i):
-            share = slice(VECTOR_COLS + GPSIMD_COLS, PAIR)
+            share = slice(sum(shares(i)), PAIR)
             nc.scalar.copy(
                 out=tiles["x_grouped", i][:, share, :].rearrange("p (n i) t -> p n t i", i=RUN),
                 in_=tiles["x_raw", i][:, :, share].rearrange("p t (n i) -> p n t i", i=RUN),
@@ -252,7 +260,8 @@ def tile_linearattention_pa_t_kernel(tc, xn, Wqkv, out_0, out_1):
             if u == 0:
                 tiles["q_out", i] = loads.tile([P, HALVES, CHUNK], F32, name="q_out")
             q_out = tiles["q_out", i]
-            nc.scalar.mul(out=q_out[:, u, :], in_=tiles["q_back", i, u][:].rearrange("p j n -> p (j n)"), mul=SCALE)
+            q_back = tiles["q_back", i, u][:].rearrange("p j n -> p (j n)")
+            nc.scalar.mul(out=q_out[:, u, :], in_=q_back, mul=SCALE)
             if u == HALVES - 1:
                 first = (i % PAIRS) * PAIR
                 nc.sync.dma_start(
@@ -260,7 +269,8 @@ def tile_linearattention_pa_t_kernel(tc, xn, Wqkv, out_0, out_1):
                 )
 
         def matmul_k_again(i, u):
-            k_again = psum.tile([P, CHUNK], F32, tag="k_again", name="k_again")
+            tag = LAST_BANKS[i % 2][u] if i >= LAST else "k_again"
+            k_again = psum.tile([P, CHUNK], F32, tag=tag, name="k_again", bufs=2 if tag == "q_t" else 1)
             channels_on_partitions(k_again, K_ROWS, i, u)
             tiles["k_again", i, u] = k_again
 
@@ -288,7 +298,8 @@ def tile_linearattention_pa_t_kernel(tc, xn, Wqkv, out_0, out_1):
 
         def copy_out_e(i):
             e_grouped = work.tile([P, HALVES, EMBED, PACK], BF16, align_bytes=64, name="e_grouped")
-            nc.scalar.copy(
+            copy = nc.vector.tensor_copy if i >= LAST else nc.scalar.copy
+            copy(
                 out=e_grouped[:].rearrange("p u m j -> p (u m j)").bitcast(F32).rearrange("p (u m w) -> p u m w", u=HALVES, w=WORDS),
                 in_=tiles["e_t", i][:].rearrange("p (u w) m -> p u m w", u=HALVES),
             )
@@ -340,17 +351,24 @@ def tile_linearattention_pa_t_kernel(tc, xn, Wqkv, out_0, out_1):
             if 0 <= i < TOTAL:
                 stage(i, *half)
 
-        for i in range(PREFETCH):
-            load_x(i)
-        for step in range(TOTAL + 5 + 5):
+        load_x(0)
+        nc.sync.dma_start(out=w_rows[:], in_=Wqkv.rearrange("(r p) c -> p r c", p=P))
+        load_x(1)
+        for step in range(TOTAL + 2):
             r = step
             a = step - 1
             q = a - 1
             c = a - 5
             run(load_x, r + PREFETCH)
+            run(sum_of_q, q - 2)
             run(quantise_v, a - 2)
             run(quantise_e, c - 2)
+            if step == 1:
+                regroup_w()
             run(quantise_x, a)
+            if step == 1:
+                quantise_w()
+            run(invert_sum_of_q, q - 2)
             run(regroup_x_gpsimd, r)
             run(regroup_x_vector, r)
             run(normalise_q, q - 2)
@@ -364,15 +382,14 @@ def tile_linearattention_pa_t_kernel(tc, xn, Wqkv, out_0, out_1):
             run(copy_out_v, a - 1, 0)
             run(regroup_x_scalar, r)
             run(matmul_v, a - 1, 1)
-            run(sum_of_q, q - 1)
             run(subtract_maximum_of_q, q, 0)
             run(matmul_q, q + 1, 0)
             run(copy_out_q, q - 3, 0)
             run(transpose_q, q - 3, 1)
             run(exp_of_k, c, 1)
             run(transpose_e, c)
-            run(matmul_k_again, c + 1, 0)
-            run(invert_sum_of_q, q - 1)
+            if c + 1 < LAST:
+                run(matmul_k_again, c + 1, 0)
             run(maximum_of_q, q, 1)
             run(maximum_of_k, a - 1, 1)
             run(matmul_k_first, a, 0)
@@ -384,3 +401,50 @@ def tile_linearattention_pa_t_kernel(tc, xn, Wqkv, out_0, out_1):
             run(copy_out_e, c)
             run(transpose_q, q - 2, 0)
             run(store_context, c - 2)
+        for i in (LAST, LAST + 1):
+            for u in range(HALVES):
+                matmul_k_again(i, u)
+        sum_of_q(TOTAL - 2)
+        quantise_e(LAST - 2)
+        invert_sum_of_q(TOTAL - 2)
+        normalise_q(TOTAL - 2)
+        quantise_e(LAST - 1)
+        matmul_context(LAST - 2)
+        matmul_context(LAST - 1)
+        for i in range(LAST, TOTAL):
+            n = i - LAST
+            for u in range(HALVES):
+                exp_of_k(i, u)
+            transpose_e(i)
+            if n == 0:
+                exp_of_q(TOTAL - 1)
+                copy_out_q(TOTAL - 3, 0)
+                transpose_q(TOTAL - 3, 1)
+            if i + 2 < TOTAL:
+                for u in range(HALVES):
+                    matmul_k_again(i + 2, u)
+            copy_out_e(i)
+            if n == 0:
+                sum_of_q(TOTAL - 1)
+                quantise_v(TOTAL - 1)
+                invert_sum_of_q(TOTAL - 1)
+                normalise_q(TOTAL - 1)
+            if n == 1:
+                copy_out_q(TOTAL - 3, 1)
+                transpose_q(TOTAL - 2, 0)
+            if n == 2:
+                copy_out_q(TOTAL - 2, 0)
+                transpose_q(TOTAL - 2, 1)
+            if n > 0:
+                quantise_e(i - 1)
+                matmul_context(i - 1)
+            if n == 1:
+                store_context(LAST - 1)
+        copy_out_q(TOTAL - 2, 1)
+        transpose_q(TOTAL - 1, 0)
+        quantise_e(TOTAL - 1)
+        copy_out_q(TOTAL - 1, 0)
+        matmul_context(TOTAL - 1)
+        transpose_q(TOTAL - 1, 1)
+        store_context(TOTAL - 1)
+        copy_out_q(TOTAL - 1, 1)

@@ -37,7 +37,7 @@ Q_ROWS, K_ROWS, V_ROWS = 0, 1, 2
 SECOND_PASS_LAG = PAIRS + 1
 PREFETCH = 2
 
-VECTOR_COLS = 64
+VECTOR_COLS = 128
 GPSIMD_COLS = 448
 
 FLOPS = 2 * 3 * EMBED * CHANNELS * POSITIONS * BATCH + 2 * BATCH * HEADS * HEAD_DIM * HEAD_DIM * POSITIONS
@@ -67,7 +67,6 @@ def tile_linearattention_pa_t_kernel(tc, xn, Wqkv, out_0, out_1):
         w_codes = const.tile([P, 3, EMBED], U32, align_bytes=64)
         w_scales = const.tile([P, 3, EMBED], U8, align_bytes=64)
         LAST = (BATCH - 1) * PAIRS
-        LAST_BANKS = (("k_again", "k_first"), ("v_t", "q_t"))
         TOTAL = BATCH * PAIRS
         tiles = {}
 
@@ -110,7 +109,7 @@ def tile_linearattention_pa_t_kernel(tc, xn, Wqkv, out_0, out_1):
 
         def regroup_w():
             for r in range(3):
-                w_t = psum.tile([P, PACK, P], BF16, tag=("e_t", "k_first", "v_t")[r], name="w_t")
+                w_t = psum.tile([P, PACK, P], BF16, tag=("e_t", "q_back", "v_t")[r], name="w_t")
                 for t in range(PACK):
                     nc.tensor.transpose(w_t[:, t, :], w_rows[:, r, t * P : (t + 1) * P], ident_bf16[:])
                 nc.scalar.copy(out=w_grouped[:, r], in_=w_t[:].rearrange("p t m -> p m t"))
@@ -158,6 +157,7 @@ def tile_linearattention_pa_t_kernel(tc, xn, Wqkv, out_0, out_1):
                 tiles["v_codes", b] = batch_pool.tile([P, CHUNKS * EMBED], U32, align_bytes=64, name="v_codes", bufs=3)
                 tiles["v_scales", b] = batch_pool.tile([P, CHUNKS * EMBED], U8, align_bytes=64, name="v_scales", bufs=3)
                 tiles["k_max", b] = batch_pool.tile([P, CHUNKS], F32, name="k_max")
+                tiles["k_rows", b] = batch_pool.tile([P, POSITIONS], F32, name="k_rows")
             first = (i % PAIRS) * PAIR
             nc.vector.quantize_mx(
                 out=tiles["x_codes", b][:, first : first + PAIR].bitcast(FP8X4),
@@ -166,16 +166,25 @@ def tile_linearattention_pa_t_kernel(tc, xn, Wqkv, out_0, out_1):
             )
 
         def matmul_k_first(i, u):
-            k_first = psum.tile([P, CHUNK], F32, tag="k_first", name="k_first")
+            k_first = psum.tile([P, CHUNK], F32, tag="k_first", name="k_first", bufs=2)
             channels_on_partitions(k_first, K_ROWS, i, u)
             tiles["k_first", i, u] = k_first
 
         def maximum_of_k(i, u):
             b, t = i // PAIRS, chunk_of(i, u)
-            nc.vector.tensor_reduce(
-                out=tiles["k_max", b][:, t : t + 1], in_=tiles["k_first", i, u][:], axis=AXIS_X, op=ALU.max
+            nc.vector.tensor_scalar(
+                out=tiles["k_rows", b][:, t * CHUNK : (t + 1) * CHUNK],
+                in0=tiles["k_first", i, u][:],
+                scalar1=0.0,
+                scalar2=None,
+                op0=ALU.add,
+                op1=ALU.max,
+                accum_out=tiles["k_max", b][:, t : t + 1],
             )
-            if t == CHUNKS - 1:
+
+        def top_of_k(i):
+            b = i // PAIRS
+            if i % PAIRS == PAIRS - 1:
                 k_top = batch_pool.tile([P, 1], F32, name="k_top")
                 nc.vector.tensor_reduce(out=k_top[:], in_=tiles["k_max", b][:], axis=AXIS_X, op=ALU.max)
                 minus_k_top = batch_pool.tile([P, 1], F32, name="minus_k_top")
@@ -250,7 +259,7 @@ def tile_linearattention_pa_t_kernel(tc, xn, Wqkv, out_0, out_1):
             tiles["q_norm", i] = q_norm
 
         def transpose_q(i, u):
-            q_back = psum.tile([P, SUBTILES, P], F32, tag="q_back", name="q_back")
+            q_back = psum.tile([P, SUBTILES, P], F32, tag="v_t" if i >= TOTAL - 3 and u == 1 else "q_back", name="q_back")
             q_tiles = tiles["q_norm", i][:].rearrange("p (u j h) c -> p u j (h c)", u=HALVES, h=HEADS)
             for j in range(SUBTILES):
                 nc.tensor.transpose(q_back[:, j, :], q_tiles[:, u, j, :], ident_f32[:])
@@ -261,28 +270,25 @@ def tile_linearattention_pa_t_kernel(tc, xn, Wqkv, out_0, out_1):
                 tiles["q_out", i] = loads.tile([P, HALVES, CHUNK], F32, name="q_out")
             q_out = tiles["q_out", i]
             q_back = tiles["q_back", i, u][:].rearrange("p j n -> p (j n)")
-            nc.scalar.mul(out=q_out[:, u, :], in_=q_back, mul=SCALE)
+            if i == TOTAL - 3:
+                nc.vector.tensor_scalar_mul(out=q_out[:, u, :], in0=q_back, scalar1=SCALE)
+            else:
+                nc.scalar.mul(out=q_out[:, u, :], in_=q_back, mul=SCALE)
             if u == HALVES - 1:
                 first = (i % PAIRS) * PAIR
                 nc.sync.dma_start(
                     out=q_soft_view[i // PAIRS, :, first : first + PAIR], in_=q_out[:].rearrange("p u n -> p (u n)")
                 )
 
-        def matmul_k_again(i, u):
-            tag = LAST_BANKS[i % 2][u] if i >= LAST else "k_again"
-            k_again = psum.tile([P, CHUNK], F32, tag=tag, name="k_again", bufs=2 if tag == "q_t" else 1)
-            channels_on_partitions(k_again, K_ROWS, i, u)
-            tiles["k_again", i, u] = k_again
-
         def exp_of_k(i, u):
             b, t = i // PAIRS, chunk_of(i, u)
             if t == 0:
                 tiles["e_sums", b] = batch_pool.tile([P, CHUNKS], F32, name="e_sums")
             if u == 0:
-                tiles["e_rows", i] = work.tile([P, HALVES, WORDS, P, 2], BF16, name="e_rows")
+                tiles["e_rows", i] = work.tile([P, HALVES, WORDS, P, 2], BF16, name="e_rows", bufs=4)
             nc.scalar.activation(
                 out=tiles["e_rows", i][:, u],
-                in_=tiles["k_again", i, u][:].rearrange("p (w i n) -> p w n i", w=WORDS, i=2),
+                in_=tiles["k_rows", b][:, t * CHUNK : (t + 1) * CHUNK].rearrange("p (w i n) -> p w n i", w=WORDS, i=2),
                 func=ACT.Exp,
                 bias=tiles["minus_k_top", b][:],
                 scale=1.0,
@@ -291,7 +297,10 @@ def tile_linearattention_pa_t_kernel(tc, xn, Wqkv, out_0, out_1):
 
         def transpose_e(i):
             e_words = tiles["e_rows", i][:].rearrange("p u w n i -> p (u w n i)").bitcast(F32)
-            e_t = psum.tile([P, HALVES * WORDS, EMBED], F32, tag="e_t", name="e_t")
+            last = i >= LAST and i % 2 == 1
+            e_t = psum.tile(
+                [P, HALVES * WORDS, EMBED], F32, tag="k_first" if last else "e_t", name="e_t", bufs=2 if last else 1
+            )
             for w in range(HALVES * WORDS):
                 nc.tensor.transpose(e_t[:, w, :], e_words[:, w * P : (w + 1) * P], ident_f32[:])
             tiles["e_t", i] = e_t
@@ -375,7 +384,6 @@ def tile_linearattention_pa_t_kernel(tc, xn, Wqkv, out_0, out_1):
             run(matmul_context, c - 2)
             run(exp_of_q, q - 1)
             run(exp_of_k, c, 0)
-            run(matmul_k_again, c, 1)
             run(maximum_of_q, q, 0)
             run(maximum_of_k, a - 1, 0)
             run(matmul_k_first, a - 1, 1)
@@ -388,22 +396,22 @@ def tile_linearattention_pa_t_kernel(tc, xn, Wqkv, out_0, out_1):
             run(transpose_q, q - 3, 1)
             run(exp_of_k, c, 1)
             run(transpose_e, c)
-            if c + 1 < LAST:
-                run(matmul_k_again, c + 1, 0)
             run(maximum_of_q, q, 1)
             run(maximum_of_k, a - 1, 1)
             run(matmul_k_first, a, 0)
             run(copy_out_v, a - 1, 1)
             run(matmul_v, a, 0)
+            run(top_of_k, a - 1)
             run(subtract_maximum_of_q, q, 1)
             run(matmul_q, q + 1, 1)
             run(copy_out_q, q - 3, 1)
             run(copy_out_e, c)
             run(transpose_q, q - 2, 0)
             run(store_context, c - 2)
-        for i in (LAST, LAST + 1):
+        exp_of_q(TOTAL - 1)
+        for i in range(LAST, TOTAL):
             for u in range(HALVES):
-                matmul_k_again(i, u)
+                exp_of_k(i, u)
         sum_of_q(TOTAL - 2)
         quantise_e(LAST - 2)
         invert_sum_of_q(TOTAL - 2)
@@ -411,40 +419,36 @@ def tile_linearattention_pa_t_kernel(tc, xn, Wqkv, out_0, out_1):
         quantise_e(LAST - 1)
         matmul_context(LAST - 2)
         matmul_context(LAST - 1)
-        for i in range(LAST, TOTAL):
-            n = i - LAST
-            for u in range(HALVES):
-                exp_of_k(i, u)
-            transpose_e(i)
-            if n == 0:
-                exp_of_q(TOTAL - 1)
-                copy_out_q(TOTAL - 3, 0)
-                transpose_q(TOTAL - 3, 1)
-            if i + 2 < TOTAL:
-                for u in range(HALVES):
-                    matmul_k_again(i + 2, u)
-            copy_out_e(i)
-            if n == 0:
-                sum_of_q(TOTAL - 1)
-                quantise_v(TOTAL - 1)
-                invert_sum_of_q(TOTAL - 1)
-                normalise_q(TOTAL - 1)
-            if n == 1:
-                copy_out_q(TOTAL - 3, 1)
-                transpose_q(TOTAL - 2, 0)
-            if n == 2:
-                copy_out_q(TOTAL - 2, 0)
-                transpose_q(TOTAL - 2, 1)
-            if n > 0:
-                quantise_e(i - 1)
-                matmul_context(i - 1)
-            if n == 1:
-                store_context(LAST - 1)
+        transpose_q(TOTAL - 3, 1)
+        copy_out_q(TOTAL - 3, 0)
+        sum_of_q(TOTAL - 1)
+        transpose_e(LAST)
+        invert_sum_of_q(TOTAL - 1)
+        normalise_q(TOTAL - 1)
+        quantise_v(TOTAL - 1)
+        copy_out_e(LAST)
+        transpose_e(LAST + 1)
+        store_context(LAST - 1)
+        copy_out_q(TOTAL - 3, 1)
+        transpose_e(LAST + 2)
+        copy_out_e(LAST + 1)
+        quantise_e(LAST)
+        transpose_q(TOTAL - 2, 0)
+        transpose_e(LAST + 3)
+        copy_out_e(LAST + 2)
+        quantise_e(LAST + 1)
+        transpose_q(TOTAL - 2, 1)
+        copy_out_q(TOTAL - 2, 0)
+        matmul_context(LAST)
         copy_out_q(TOTAL - 2, 1)
+        copy_out_e(LAST + 3)
+        quantise_e(LAST + 2)
         transpose_q(TOTAL - 1, 0)
-        quantise_e(TOTAL - 1)
-        copy_out_q(TOTAL - 1, 0)
-        matmul_context(TOTAL - 1)
         transpose_q(TOTAL - 1, 1)
-        store_context(TOTAL - 1)
+        matmul_context(LAST + 1)
+        copy_out_q(TOTAL - 1, 0)
         copy_out_q(TOTAL - 1, 1)
+        matmul_context(LAST + 2)
+        quantise_e(LAST + 3)
+        matmul_context(LAST + 3)
+        store_context(TOTAL - 1)

@@ -105,7 +105,7 @@ def tile_linearattention_pa_t_kernel(tc, xn, Wqkv, out_0, out_1):
             tiles["x_raw", i] = x_raw
 
         def shares(i):
-            return (448, 320) if i < 2 else (VECTOR_COLS, GPSIMD_COLS)
+            return (384, 256) if i < 2 else (VECTOR_COLS, GPSIMD_COLS)
 
         def regroup_w():
             for r in range(3):
@@ -156,8 +156,6 @@ def tile_linearattention_pa_t_kernel(tc, xn, Wqkv, out_0, out_1):
                 tiles["x_scales", b] = batch_pool.tile([P, POSITIONS], U8, align_bytes=64, name="x_scales")
                 tiles["v_codes", b] = batch_pool.tile([P, CHUNKS * EMBED], U32, align_bytes=64, name="v_codes", bufs=3)
                 tiles["v_scales", b] = batch_pool.tile([P, CHUNKS * EMBED], U8, align_bytes=64, name="v_scales", bufs=3)
-                tiles["k_max", b] = batch_pool.tile([P, CHUNKS], F32, name="k_max")
-                tiles["k_rows", b] = batch_pool.tile([P, POSITIONS], F32, name="k_rows")
             first = (i % PAIRS) * PAIR
             nc.vector.quantize_mx(
                 out=tiles["x_codes", b][:, first : first + PAIR].bitcast(FP8X4),
@@ -172,23 +170,24 @@ def tile_linearattention_pa_t_kernel(tc, xn, Wqkv, out_0, out_1):
 
         def maximum_of_k(i, u):
             b, t = i // PAIRS, chunk_of(i, u)
+            if t == 0:
+                tiles["k_low", b] = batch_pool.tile([P, CHUNKS], F32, name="k_low")
+                tiles["minus_k", b] = batch_pool.tile([P, POSITIONS], F32, name="minus_k")
             nc.vector.tensor_scalar(
-                out=tiles["k_rows", b][:, t * CHUNK : (t + 1) * CHUNK],
+                out=tiles["minus_k", b][:, t * CHUNK : (t + 1) * CHUNK],
                 in0=tiles["k_first", i, u][:],
-                scalar1=0.0,
+                scalar1=-1.0,
                 scalar2=None,
-                op0=ALU.add,
-                op1=ALU.max,
-                accum_out=tiles["k_max", b][:, t : t + 1],
+                op0=ALU.mult,
+                op1=ALU.min,
+                accum_out=tiles["k_low", b][:, t : t + 1],
             )
 
         def top_of_k(i):
             b = i // PAIRS
             if i % PAIRS == PAIRS - 1:
-                k_top = batch_pool.tile([P, 1], F32, name="k_top")
-                nc.vector.tensor_reduce(out=k_top[:], in_=tiles["k_max", b][:], axis=AXIS_X, op=ALU.max)
                 minus_k_top = batch_pool.tile([P, 1], F32, name="minus_k_top")
-                nc.vector.tensor_scalar_mul(out=minus_k_top[:], in0=k_top[:], scalar1=-1.0)
+                nc.vector.tensor_reduce(out=minus_k_top[:], in_=tiles["k_low", b][:], axis=AXIS_X, op=ALU.min)
                 tiles["minus_k_top", b] = minus_k_top
 
         def matmul_v(i, u):
@@ -280,19 +279,18 @@ def tile_linearattention_pa_t_kernel(tc, xn, Wqkv, out_0, out_1):
                     out=q_soft_view[i // PAIRS, :, first : first + PAIR], in_=q_out[:].rearrange("p u n -> p (u n)")
                 )
 
-        def exp_of_k(i, u):
-            b, t = i // PAIRS, chunk_of(i, u)
-            if t == 0:
-                tiles["e_sums", b] = batch_pool.tile([P, CHUNKS], F32, name="e_sums")
-            if u == 0:
-                tiles["e_rows", i] = work.tile([P, HALVES, WORDS, P, 2], BF16, name="e_rows", bufs=4)
+        def exp_of_k(i):
+            b, first = i // PAIRS, (i % PAIRS) * PAIR
+            if i % PAIRS == 0:
+                tiles["e_sums", b] = batch_pool.tile([P, PAIRS], F32, name="e_sums")
+            tiles["e_rows", i] = work.tile([P, HALVES, WORDS, P, 2], BF16, name="e_rows", bufs=4)
             nc.scalar.activation(
-                out=tiles["e_rows", i][:, u],
-                in_=tiles["k_rows", b][:, t * CHUNK : (t + 1) * CHUNK].rearrange("p (w i n) -> p w n i", w=WORDS, i=2),
+                out=tiles["e_rows", i][:].rearrange("p u w n i -> p (u w) n i"),
+                in_=tiles["minus_k", b][:, first : first + PAIR].rearrange("p (w i n) -> p w n i", w=HALVES * WORDS, i=2),
                 func=ACT.Exp,
                 bias=tiles["minus_k_top", b][:],
-                scale=1.0,
-                accum_out=tiles["e_sums", b][:, t : t + 1],
+                scale=-1.0,
+                accum_out=tiles["e_sums", b][:, i % PAIRS : i % PAIRS + 1],
             )
 
         def transpose_e(i):
@@ -340,21 +338,29 @@ def tile_linearattention_pa_t_kernel(tc, xn, Wqkv, out_0, out_1):
                     stop=(t == CHUNKS - 1),
                 )
 
+        def ends_batch(i):
+            return i % PAIRS == PAIRS - 1
+
+        def total_of_e(i):
+            if ends_batch(i):
+                e_total = batch_pool.tile([P, 1], F32, name="e_total")
+                nc.vector.tensor_reduce(out=e_total[:], in_=tiles["e_sums", i // PAIRS][:], axis=AXIS_X, op=ALU.add)
+                tiles["e_total", i] = e_total
+
+        def invert_total_of_e(i):
+            if ends_batch(i):
+                e_inv = batch_pool.tile([P, 1], F32, name="e_inv")
+                nc.vector.reciprocal(out=e_inv[:], in_=tiles["e_total", i][:])
+                tiles["e_inv", i] = e_inv
+
         def store_context(i):
-            b = i // PAIRS
-            if i % PAIRS != PAIRS - 1:
-                return
-            e_total = batch_pool.tile([P, 1], F32, name="e_total")
-            nc.vector.tensor_reduce(out=e_total[:], in_=tiles["e_sums", b][:], axis=AXIS_X, op=ALU.add)
-            e_inv = batch_pool.tile([P, 1], F32, name="e_inv")
-            nc.vector.reciprocal(out=e_inv[:], in_=e_total[:])
-            context_out = batch_pool.tile([P, HEAD_DIM], F32, name="context_out")
-            for h in range(HEADS):
-                rows = slice(h * HEAD_DIM, (h + 1) * HEAD_DIM)
-                nc.vector.tensor_scalar_mul(
-                    out=context_out[rows, :], in0=tiles["context", b][rows, rows], scalar1=e_inv[rows, :]
-                )
-            nc.sync.dma_start(out=context_view[b], in_=context_out[:])
+            if ends_batch(i):
+                b = i // PAIRS
+                context_out = batch_pool.tile([P, EMBED], F32, name="context_out")
+                nc.vector.tensor_scalar_mul(out=context_out[:], in0=tiles["context", b][:], scalar1=tiles["e_inv", i][:])
+                for h in range(HEADS):
+                    rows = slice(h * HEAD_DIM, (h + 1) * HEAD_DIM)
+                    nc.sync.dma_start(out=context_view[b, rows, :], in_=context_out[rows, rows])
 
         def run(stage, i, *half):
             if 0 <= i < TOTAL:
@@ -370,11 +376,13 @@ def tile_linearattention_pa_t_kernel(tc, xn, Wqkv, out_0, out_1):
             c = a - 5
             run(load_x, r + PREFETCH)
             run(sum_of_q, q - 2)
-            run(quantise_v, a - 2)
+            run(total_of_e, c - 2)
+            run(invert_total_of_e, c - 2)
             run(quantise_e, c - 2)
             if step == 1:
                 regroup_w()
             run(quantise_x, a)
+            run(quantise_v, a - 2)
             if step == 1:
                 quantise_w()
             run(invert_sum_of_q, q - 2)
@@ -383,7 +391,6 @@ def tile_linearattention_pa_t_kernel(tc, xn, Wqkv, out_0, out_1):
             run(normalise_q, q - 2)
             run(matmul_context, c - 2)
             run(exp_of_q, q - 1)
-            run(exp_of_k, c, 0)
             run(maximum_of_q, q, 0)
             run(maximum_of_k, a - 1, 0)
             run(matmul_k_first, a - 1, 1)
@@ -393,16 +400,16 @@ def tile_linearattention_pa_t_kernel(tc, xn, Wqkv, out_0, out_1):
             run(subtract_maximum_of_q, q, 0)
             run(matmul_q, q + 1, 0)
             run(copy_out_q, q - 3, 0)
+            run(exp_of_k, c)
             run(transpose_q, q - 3, 1)
-            run(exp_of_k, c, 1)
             run(transpose_e, c)
             run(maximum_of_q, q, 1)
             run(maximum_of_k, a - 1, 1)
             run(matmul_k_first, a, 0)
             run(copy_out_v, a - 1, 1)
             run(matmul_v, a, 0)
-            run(top_of_k, a - 1)
             run(subtract_maximum_of_q, q, 1)
+            run(top_of_k, a - 1)
             run(matmul_q, q + 1, 1)
             run(copy_out_q, q - 3, 1)
             run(copy_out_e, c)
@@ -410,10 +417,11 @@ def tile_linearattention_pa_t_kernel(tc, xn, Wqkv, out_0, out_1):
             run(store_context, c - 2)
         exp_of_q(TOTAL - 1)
         for i in range(LAST, TOTAL):
-            for u in range(HALVES):
-                exp_of_k(i, u)
+            exp_of_k(i)
         sum_of_q(TOTAL - 2)
+        total_of_e(LAST - 1)
         quantise_e(LAST - 2)
+        invert_total_of_e(LAST - 1)
         invert_sum_of_q(TOTAL - 2)
         normalise_q(TOTAL - 2)
         quantise_e(LAST - 1)
@@ -442,7 +450,9 @@ def tile_linearattention_pa_t_kernel(tc, xn, Wqkv, out_0, out_1):
         matmul_context(LAST)
         copy_out_q(TOTAL - 2, 1)
         copy_out_e(LAST + 3)
+        total_of_e(TOTAL - 1)
         quantise_e(LAST + 2)
+        invert_total_of_e(TOTAL - 1)
         transpose_q(TOTAL - 1, 0)
         transpose_q(TOTAL - 1, 1)
         matmul_context(LAST + 1)

from contextlib import ExitStack

import concourse.mybir as mybir
from concourse.masks import make_identity

BF16 = mybir.dt.bfloat16
F32 = mybir.dt.float32
U32 = mybir.dt.uint32
U8 = mybir.dt.uint8
FP8X4 = mybir.dt.float8_e4m3fn_x4
ALU = mybir.AluOpType
ACT = mybir.ActivationFunctionType
AXIS_X = mybir.AxisListType.X

P = 128
PACK = 4
BATCH = 4
CHANNELS = 512
POSITIONS = 4096
EMBED = 128
HEADS = 4
HEAD_DIM = 32
SCALE = HEAD_DIM**-0.5

CHUNK = 512
CHUNKS = POSITIONS // CHUNK
SUBTILES = CHUNK // P
GROUPS = SUBTILES * HEADS
HALVES = 2
PAIR = HALVES * CHUNK
PAIRS = POSITIONS // PAIR
WORDS = SUBTILES // 2
RUN = 4

Q_ROWS, K_ROWS, V_ROWS = 0, 1, 2

SECOND_PASS_LAG = PAIRS + 1
PREFETCH = 2

VECTOR_COLS = 128
GPSIMD_COLS = 448

FLOPS = 2 * 3 * EMBED * CHANNELS * POSITIONS * BATCH + 2 * BATCH * HEADS * HEAD_DIM * HEAD_DIM * POSITIONS


def tile_linearattention_pa_t_kernel(tc, xn, Wqkv, out_0, out_1):
    nc = tc.nc
    xn_view = xn.rearrange("b (t p) h w -> b p t (h w)", p=P)
    q_soft_view = out_0.rearrange("b h c n -> b (h c) n")
    context_view = out_1.rearrange("b h d f -> b (h d) f")

    with ExitStack() as stack:
        const = stack.enter_context(tc.tile_pool(name="const", bufs=1))
        loads = stack.enter_context(tc.tile_pool(name="loads", bufs=4))
        work = stack.enter_context(tc.tile_pool(name="work", bufs=3))
        batch_pool = stack.enter_context(tc.tile_pool(name="batch", bufs=2))
        psum = stack.enter_context(tc.psum_pool(name="psum", bufs=1))
        stack.enter_context(tc.manual_schedule())

        ident_bf16 = const.tile([P, P], BF16)
        make_identity(nc, ident_bf16[:])
        ident_f32 = const.tile([P, P], F32)
        make_identity(nc, ident_f32[:])

        w_rows = const.tile([P, 3, CHANNELS], BF16)
        w_grouped = const.tile([P, 3, EMBED, PACK], BF16, align_bytes=64)
        w_codes = const.tile([P, 3, EMBED], U32, align_bytes=64)
        w_scales = const.tile([P, 3, EMBED], U8, align_bytes=64)
        LAST = (BATCH - 1) * PAIRS
        TOTAL = BATCH * PAIRS
        tiles = {}

        def chunk_of(i, u):
            return (i % PAIRS) * HALVES + u

        def channels_on_partitions(bank, rows, i, u):
            first = chunk_of(i, u) * CHUNK
            nc.tensor.matmul_mx(
                out=bank[:],
                lhsT=w_codes[:, rows, :].bitcast(FP8X4),
                lhsT_scale=w_scales[:, rows, :],
                rhs=tiles["x_codes", i // PAIRS][:, first : first + CHUNK].bitcast(FP8X4),
                rhs_scale=tiles["x_scales", i // PAIRS][:, first : first + CHUNK],
                start=True,
                stop=True,
            )

        def positions_on_partitions(bank, rows, i, u):
            for j in range(SUBTILES):
                first = chunk_of(i, u) * CHUNK + j * P
                nc.tensor.matmul_mx(
                    out=bank[:, j, :],
                    lhsT=tiles["x_codes", i // PAIRS][:, first : first + P].bitcast(FP8X4),
                    lhsT_scale=tiles["x_scales", i // PAIRS][:, first : first + P],
                    rhs=w_codes[:, rows, :].bitcast(FP8X4),
                    rhs_scale=w_scales[:, rows, :],
                    start=True,
                    stop=True,
                )

        def load_x(i):
            first = (i % PAIRS) * PAIR
            x_raw = loads.tile([P, PACK, PAIR], BF16, name="x_raw")
            nc.sync.dma_start(out=x_raw[:], in_=xn_view[i // PAIRS, :, :, first : first + PAIR])
            tiles["x_raw", i] = x_raw

        def shares(i):
            return (384, 256) if i < 2 else (VECTOR_COLS, GPSIMD_COLS)

        def regroup_w():
            for r in range(3):
                w_t = psum.tile([P, PACK, P], BF16, tag=("e_t", "q_back", "v_t")[r], name="w_t")
                for t in range(PACK):
                    nc.tensor.transpose(w_t[:, t, :], w_rows[:, r, t * P : (t + 1) * P], ident_bf16[:])
                nc.scalar.copy(out=w_grouped[:, r], in_=w_t[:].rearrange("p t m -> p m t"))

        def quantise_w():
            for r in range(3):
                nc.vector.quantize_mx(
                    out=w_codes[:, r, :].bitcast(FP8X4),
                    scales=w_scales[:, r, :],
                    in_=w_grouped[:, r].rearrange("p m t -> p (m t)"),
                )

        def regroup_x_gpsimd(i):
            x_grouped = work.tile([P, PAIR, PACK], BF16, align_bytes=64, name="x_grouped", bufs=1)
            tiles["x_grouped", i] = x_grouped
            share = slice(shares(i)[0], sum(shares(i)))
            nc.gpsimd.tensor_scalar(
                out=x_grouped[:, share, :],
                in0=tiles["x_raw", i][:, :, share].rearrange("p t n -> p n t"),
                scalar1=1.0,
                scalar2=0.0,
                op0=ALU.mult,
                op1=ALU.add,
            )

        def regroup_x_vector(i):
            share = slice(0, shares(i)[0])
            nc.vector.tensor_copy(
                out=tiles["x_grouped", i][:, share, :].rearrange("p (n i) t -> p n t i", i=RUN),
                in_=tiles["x_raw", i][:, :, share].rearrange("p t (n i) -> p n t i", i=RUN),
            )

        def regroup_x_scalar(i):
            share = slice(sum(shares(i)), PAIR)
            nc.scalar.copy(
                out=tiles["x_grouped", i][:, share, :].rearrange("p (n i) t -> p n t i", i=RUN),
                in_=tiles["x_raw", i][:, :, share].rearrange("p t (n i) -> p n t i", i=RUN),
            )

        def quantise_x(i):
            b = i // PAIRS
            if i % PAIRS == 0:
                tiles["x_codes", b] = batch_pool.tile([P, POSITIONS], U32, align_bytes=64, name="x_codes")
                tiles["x_scales", b] = batch_pool.tile([P, POSITIONS], U8, align_bytes=64, name="x_scales")
                tiles["v_codes", b] = batch_pool.tile([P, CHUNKS * EMBED], U32, align_bytes=64, name="v_codes", bufs=3)
                tiles["v_scales", b] = batch_pool.tile([P, CHUNKS * EMBED], U8, align_bytes=64, name="v_scales", bufs=3)
            first = (i % PAIRS) * PAIR
            nc.vector.quantize_mx(
                out=tiles["x_codes", b][:, first : first + PAIR].bitcast(FP8X4),
                scales=tiles["x_scales", b][:, first : first + PAIR],
                in_=tiles["x_grouped", i][:].rearrange("p n t -> p (n t)"),
            )

        def matmul_k_first(i, u):
            k_first = psum.tile([P, CHUNK], F32, tag="k_first", name="k_first", bufs=2)
            channels_on_partitions(k_first, K_ROWS, i, u)
            tiles["k_first", i, u] = k_first

        def maximum_of_k(i, u):
            b, t = i // PAIRS, chunk_of(i, u)
            if t == 0:
                tiles["k_low", b] = batch_pool.tile([P, CHUNKS], F32, name="k_low")
                tiles["minus_k", b] = batch_pool.tile([P, POSITIONS], F32, name="minus_k")
            nc.vector.tensor_scalar(
                out=tiles["minus_k", b][:, t * CHUNK : (t + 1) * CHUNK],
                in0=tiles["k_first", i, u][:],
                scalar1=-1.0,
                scalar2=None,
                op0=ALU.mult,
                op1=ALU.min,
                accum_out=tiles["k_low", b][:, t : t + 1],
            )

        def top_of_k(i):
            b = i // PAIRS
            if i % PAIRS == PAIRS - 1:
                minus_k_top = batch_pool.tile([P, 1], F32, name="minus_k_top")
                nc.vector.tensor_reduce(out=minus_k_top[:], in_=tiles["k_low", b][:], axis=AXIS_X, op=ALU.min)
                tiles["minus_k_top", b] = minus_k_top

        def matmul_v(i, u):
            v_t = psum.tile([P, SUBTILES, EMBED], F32, tag="v_t", name="v_t")
            positions_on_partitions(v_t, V_ROWS, i, u)
            tiles["v_t", i, u] = v_t

        def copy_out_v(i, u):
            if u == 0:
                tiles["v_grouped", i] = work.tile([P, HALVES, EMBED, PACK], BF16, align_bytes=64, name="v_grouped")
            nc.scalar.copy(out=tiles["v_grouped", i][:, u], in_=tiles["v_t", i, u][:].rearrange("p j m -> p m j"))

        def quantise_v(i):
            b = i // PAIRS
            first = chunk_of(i, 0) * EMBED
            nc.vector.quantize_mx(
                out=tiles["v_codes", b][:, first : first + HALVES * EMBED].bitcast(FP8X4),
                scales=tiles["v_scales", b][:, first : first + HALVES * EMBED],
                in_=tiles["v_grouped", i][:].rearrange("p u m j -> p (u m j)"),
            )

        def spread(per_group):
            return per_group.unsqueeze(2).to_broadcast([P, per_group.shape[1], HEAD_DIM])

        def matmul_q(i, u):
            q_t = psum.tile([P, SUBTILES, EMBED], F32, tag="q_t", bufs=2, name="q_t")
            positions_on_partitions(q_t, Q_ROWS, i, u)
            tiles["q_t", i, u] = q_t[:].rearrange("p j (h c) -> p (j h) c", c=HEAD_DIM)

        def maximum_of_q(i, u):
            if u == 0:
                tiles["q_max", i] = work.tile([P, HALVES, GROUPS], F32, name="q_max")
            nc.vector.tensor_reduce(out=tiles["q_max", i][:, u, :], in_=tiles["q_t", i, u], axis=AXIS_X, op=ALU.max)

        def subtract_maximum_of_q(i, u):
            if u == 0:
                tiles["q_exp", i] = work.tile([P, HALVES, GROUPS, HEAD_DIM], F32, name="q_exp", bufs=4)
            nc.vector.tensor_tensor(
                out=tiles["q_exp", i][:, u],
                in0=tiles["q_t", i, u],
                in1=spread(tiles["q_max", i][:, u, :]),
                op=ALU.subtract,
            )

        def exp_of_q(i):
            nc.scalar.activation(out=tiles["q_exp", i][:], in_=tiles["q_exp", i][:], func=ACT.Exp)

        def sum_of_q(i):
            q_sum = work.tile([P, HALVES * GROUPS], F32, name="q_sum")
            nc.vector.tensor_reduce(
                out=q_sum[:], in_=tiles["q_exp", i][:].rearrange("p u g c -> p (u g) c"), axis=AXIS_X, op=ALU.add
            )
            tiles["q_sum", i] = q_sum

        def invert_sum_of_q(i):
            q_inv = work.tile([P, HALVES * GROUPS], F32, name="q_inv")
            nc.vector.reciprocal(out=q_inv[:], in_=tiles["q_sum", i][:])
            tiles["q_inv", i] = q_inv

        def normalise_q(i):
            q_norm = work.tile([P, HALVES * GROUPS, HEAD_DIM], F32, name="q_norm")
            nc.gpsimd.tensor_tensor(
                out=q_norm[:],
                in0=tiles["q_exp", i][:].rearrange("p u g c -> p (u g) c"),
                in1=spread(tiles["q_inv", i][:]),
                op=ALU.mult,
            )
            tiles["q_norm", i] = q_norm

        def transpose_q(i, u):
            q_back = psum.tile([P, SUBTILES, P], F32, tag="v_t" if i >= TOTAL - 3 and u == 1 else "q_back", name="q_back")
            q_tiles = tiles["q_norm", i][:].rearrange("p (u j h) c -> p u j (h c)", u=HALVES, h=HEADS)
            for j in range(SUBTILES):
                nc.tensor.transpose(q_back[:, j, :], q_tiles[:, u, j, :], ident_f32[:])
            tiles["q_back", i, u] = q_back

        def copy_out_q(i, u):
            if u == 0:
                tiles["q_out", i] = loads.tile([P, HALVES, CHUNK], F32, name="q_out")
            q_out = tiles["q_out", i]
            q_back = tiles["q_back", i, u][:].rearrange("p j n -> p (j n)")
            if i == TOTAL - 3:
                nc.vector.tensor_scalar_mul(out=q_out[:, u, :], in0=q_back, scalar1=SCALE)
            else:
                nc.scalar.mul(out=q_out[:, u, :], in_=q_back, mul=SCALE)
            if u == HALVES - 1:
                first = (i % PAIRS) * PAIR
                nc.sync.dma_start(
                    out=q_soft_view[i // PAIRS, :, first : first + PAIR], in_=q_out[:].rearrange("p u n -> p (u n)")
                )

        def exp_of_k(i):
            b, first = i // PAIRS, (i % PAIRS) * PAIR
            if i % PAIRS == 0:
                tiles["e_sums", b] = batch_pool.tile([P, PAIRS], F32, name="e_sums")
            tiles["e_rows", i] = work.tile([P, HALVES, WORDS, P, 2], BF16, name="e_rows", bufs=4)
            nc.scalar.activation(
                out=tiles["e_rows", i][:].rearrange("p u w n i -> p (u w) n i"),
                in_=tiles["minus_k", b][:, first : first + PAIR].rearrange("p (w i n) -> p w n i", w=HALVES * WORDS, i=2),
                func=ACT.Exp,
                bias=tiles["minus_k_top", b][:],
                scale=-1.0,
                accum_out=tiles["e_sums", b][:, i % PAIRS : i % PAIRS + 1],
            )

        def transpose_e(i):
            e_words = tiles["e_rows", i][:].rearrange("p u w n i -> p (u w n i)").bitcast(F32)
            last = i >= LAST and i % 2 == 1
            e_t = psum.tile(
                [P, HALVES * WORDS, EMBED], F32, tag="k_first" if last else "e_t", name="e_t", bufs=2 if last else 1
            )
            for w in range(HALVES * WORDS):
                nc.tensor.transpose(e_t[:, w, :], e_words[:, w * P : (w + 1) * P], ident_f32[:])
            tiles["e_t", i] = e_t

        def copy_out_e(i):
            e_grouped = work.tile([P, HALVES, EMBED, PACK], BF16, align_bytes=64, name="e_grouped")
            copy = nc.vector.tensor_copy if i >= LAST else nc.scalar.copy
            copy(
                out=e_grouped[:].rearrange("p u m j -> p (u m j)").bitcast(F32).rearrange("p (u m w) -> p u m w", u=HALVES, w=WORDS),
                in_=tiles["e_t", i][:].rearrange("p (u w) m -> p u m w", u=HALVES),
            )
            tiles["e_grouped", i] = e_grouped

        def quantise_e(i):
            e_codes = work.tile([P, HALVES, EMBED], U32, align_bytes=64, name="e_codes")
            e_scales = work.tile([P, HALVES, EMBED], U8, align_bytes=64, name="e_scales")
            nc.vector.quantize_mx(
                out=e_codes[:].rearrange("p u m -> p (u m)").bitcast(FP8X4),
                scales=e_scales[:].rearrange("p u m -> p (u m)"),
                in_=tiles["e_grouped", i][:].rearrange("p u m j -> p (u m j)"),
            )
            tiles["e_codes", i], tiles["e_scales", i] = e_codes, e_scales

        def matmul_context(i):
            b = i // PAIRS
            if i % PAIRS == 0:
                tiles["context", b] = psum.tile([P, EMBED], F32, tag="context", name="context")
            for u in range(HALVES):
                t = chunk_of(i, u)
                nc.tensor.matmul_mx(
                    out=tiles["context", b][:],
                    lhsT=tiles["e_codes", i][:, u, :].bitcast(FP8X4),
                    lhsT_scale=tiles["e_scales", i][:, u, :],
                    rhs=tiles["v_codes", b][:, t * EMBED : (t + 1) * EMBED].bitcast(FP8X4),
                    rhs_scale=tiles["v_scales", b][:, t * EMBED : (t + 1) * EMBED],
                    start=(t == 0),
                    stop=(t == CHUNKS - 1),
                )

        def ends_batch(i):
            return i % PAIRS == PAIRS - 1

        def total_of_e(i):
            if ends_batch(i):
                e_total = batch_pool.tile([P, 1], F32, name="e_total")
                nc.vector.tensor_reduce(out=e_total[:], in_=tiles["e_sums", i // PAIRS][:], axis=AXIS_X, op=ALU.add)
                tiles["e_total", i] = e_total

        def invert_total_of_e(i):
            if ends_batch(i):
                e_inv = batch_pool.tile([P, 1], F32, name="e_inv")
                nc.vector.reciprocal(out=e_inv[:], in_=tiles["e_total", i][:])
                tiles["e_inv", i] = e_inv

        def store_context(i):
            if ends_batch(i):
                b = i // PAIRS
                context_out = batch_pool.tile([P, EMBED], F32, name="context_out")
                nc.vector.tensor_scalar_mul(out=context_out[:], in0=tiles["context", b][:], scalar1=tiles["e_inv", i][:])
                for h in range(HEADS):
                    rows = slice(h * HEAD_DIM, (h + 1) * HEAD_DIM)
                    nc.sync.dma_start(out=context_view[b, rows, :], in_=context_out[rows, rows])

        def run(stage, i, *half):
            if 0 <= i < TOTAL:
                stage(i, *half)

        load_x(0)
        nc.sync.dma_start(out=w_rows[:], in_=Wqkv.rearrange("(r p) c -> p r c", p=P))
        load_x(1)
        for step in range(TOTAL + 2):
            r = step
            a = step - 1
            q = a - 1
            c = a - 5
            run(load_x, r + PREFETCH)
            run(sum_of_q, q - 2)
            run(total_of_e, c - 2)
            run(invert_total_of_e, c - 2)
            run(quantise_e, c - 2)
            if step == 1:
                regroup_w()
            run(quantise_x, a)
            run(quantise_v, a - 2)
            if step == 1:
                quantise_w()
            run(invert_sum_of_q, q - 2)
            run(regroup_x_gpsimd, r)
            run(regroup_x_vector, r)
            run(normalise_q, q - 2)
            run(matmul_context, c - 2)
            run(exp_of_q, q - 1)
            run(maximum_of_q, q, 0)
            run(maximum_of_k, a - 1, 0)
            run(matmul_k_first, a - 1, 1)
            run(copy_out_v, a - 1, 0)
            run(regroup_x_scalar, r)
            run(matmul_v, a - 1, 1)
            run(subtract_maximum_of_q, q, 0)
            run(matmul_q, q + 1, 0)
            run(copy_out_q, q - 3, 0)
            run(exp_of_k, c)
            run(transpose_q, q - 3, 1)
            run(transpose_e, c)
            run(maximum_of_q, q, 1)
            run(maximum_of_k, a - 1, 1)
            run(matmul_k_first, a, 0)
            run(copy_out_v, a - 1, 1)
            run(matmul_v, a, 0)
            run(subtract_maximum_of_q, q, 1)
            run(top_of_k, a - 1)
            run(matmul_q, q + 1, 1)
            run(copy_out_q, q - 3, 1)
            run(copy_out_e, c)
            run(transpose_q, q - 2, 0)
            run(store_context, c - 2)
        exp_of_q(TOTAL - 1)
        for i in range(LAST, TOTAL):
            exp_of_k(i)
        sum_of_q(TOTAL - 2)
        total_of_e(LAST - 1)
        quantise_e(LAST - 2)
        invert_total_of_e(LAST - 1)
        invert_sum_of_q(TOTAL - 2)
        normalise_q(TOTAL - 2)
        quantise_e(LAST - 1)
        matmul_context(LAST - 2)
        matmul_context(LAST - 1)
        transpose_q(TOTAL - 3, 1)
        copy_out_q(TOTAL - 3, 0)
        sum_of_q(TOTAL - 1)
        transpose_e(LAST)
        invert_sum_of_q(TOTAL - 1)
        normalise_q(TOTAL - 1)
        quantise_v(TOTAL - 1)
        copy_out_e(LAST)
        transpose_e(LAST + 1)
        store_context(LAST - 1)
        copy_out_q(TOTAL - 3, 1)
        transpose_e(LAST + 2)
        copy_out_e(LAST + 1)
        quantise_e(LAST)
        transpose_q(TOTAL - 2, 0)
        transpose_e(LAST + 3)
        copy_out_e(LAST + 2)
        quantise_e(LAST + 1)
        transpose_q(TOTAL - 2, 1)
        copy_out_q(TOTAL - 2, 0)
        matmul_context(LAST)
        copy_out_q(TOTAL - 2, 1)
        copy_out_e(LAST + 3)
        total_of_e(TOTAL - 1)
        quantise_e(LAST + 2)
        invert_total_of_e(TOTAL - 1)
        transpose_q(TOTAL - 1, 0)
        transpose_q(TOTAL - 1, 1)
        matmul_context(LAST + 1)
        copy_out_q(TOTAL - 1, 0)
        copy_out_q(TOTAL - 1, 1)
        matmul_context(LAST + 2)
        quantise_e(LAST + 3)
        matmul_context(LAST + 3)
        store_context(TOTAL - 1)
